import numpy as np
import ml_dtypes


def mxq(x, axis, fmt="e4m3"):
    dtype, down = {"e4m3": (ml_dtypes.float8_e4m3fn, 7), "e5m2": (ml_dtypes.float8_e5m2, 14)}[fmt]
    v = np.moveaxis(np.asarray(x, np.float32).astype(ml_dtypes.bfloat16).astype(np.float64), axis, -1)
    blocks = v.reshape(v.shape[:-1] + (-1, 32))
    amax = np.abs(blocks).max(-1, keepdims=True)
    byte = np.maximum(np.where(amax > 0, np.frexp(amax)[1] - 1 + 127, 0) - down, 1)
    scale = np.exp2(byte - 127.0)
    codes = (blocks / scale).astype(np.float32).astype(dtype).astype(np.float64)
    return np.moveaxis((codes * scale).reshape(v.shape), -1, axis)


WIDE = False


def mx_kscale(k):
    if not WIDE:
        return np.ones(k)
    levels = np.array([10, -10, 5, -5, 0])
    a = np.random.permutation(np.resize(levels, k // 512 * 4)).reshape(k // 512, 4)
    idx = np.arange(k)
    return np.exp2(a[idx // 512, idx % 128 // 32])


BF16 = ml_dtypes.bfloat16


def bf(x):
    return np.asarray(x, np.float32).astype(BF16)


def f64(x):
    return np.asarray(x).astype(np.float64)


B, S, H, N, L = 2, 1024, 1024, 1024, 10
EPS = 1e-06


def setup_inputs():
    s = mx_kscale(H)
    return {"hidden_states": bf(np.random.standard_normal((B, S, H)) * s),
            "conv_w": bf(np.random.standard_normal((L, N, H)) / np.sqrt(H) / s),
            "norm_w": bf(1.0 + 0.1 * np.random.standard_normal(N))}


def reference(hidden_states, conv_w, norm_w):
    x = f64(hidden_states)
    w_sum = f64(conv_w).sum(axis=0)
    out = (mxq(x, 2, "e4m3") @ mxq(w_sum, 1, "e4m3").T) / L
    norm_x = np.sqrt(np.sum(out * out, axis=-1, keepdims=True) + EPS * H)
    x_normed = out / norm_x * np.sqrt(H)
    return x_normed * f64(norm_w)

@@ -1,0 +1,199 @@
+from contextlib import ExitStack
+
+import concourse.mybir as mybir
+from concourse.masks import make_identity
+
+F32 = mybir.dt.float32
+BF16 = mybir.dt.bfloat16
+U32 = mybir.dt.uint32
+U8 = mybir.dt.uint8
+FP8X4 = mybir.dt.float8_e4m3fn_x4
+ALU = mybir.AluOpType
+ACT = mybir.ActivationFunctionType
+
+P = 128
+H = 1024
+N = 1024
+L = 10
+TOKENS = 2048
+EPS = 1e-06
+FLOPS = 2 * TOKENS * H * N
+
+S_PAIRS = (0,)
+
+
+def perm_read(ap):
+    return ap.rearrange("p (c q e) -> p c e q", c=8, q=128, e=2)
+
+
+def split_write(ap):
+    return ap.rearrange("p (c e q) -> p c e q", c=8, q=128, e=2)
+
+
+def tile_conv2dlinalgrmsnorm_kernel(tc, hidden_states, conv_w, norm_w, out):
+    nc = tc.nc
+    x_flat = hidden_states.flatten_outer_dims()
+    out_flat = out.flatten_outer_dims()
+    with ExitStack() as ctx:
+        const = ctx.enter_context(tc.tile_pool(name="const", bufs=1))
+        rawp = ctx.enter_context(tc.tile_pool(name="rawp", bufs=8))
+        bigp = ctx.enter_context(tc.tile_pool(name="bigp", bufs=10))
+        grpp = ctx.enter_context(tc.tile_pool(name="grpp", bufs=4))
+        xcp = ctx.enter_context(tc.tile_pool(name="xcp", bufs=16))
+        junkp = ctx.enter_context(tc.tile_pool(name="junkp", bufs=2))
+        small = ctx.enter_context(tc.tile_pool(name="small", bufs=4))
+        psum = ctx.enter_context(tc.psum_pool(name="psum", bufs=8))
+
+        warm_in = const.tile([P, 1], F32)
+        nc.vector.memset(warm_in[:], 1.0)
+        warm_out = const.tile([P, 1], F32)
+        nc.scalar.activation(out=warm_out[:], in_=warm_in[:], func=ACT.Sqrt)
+
+        ident = const.tile([P, P], F32)
+        make_identity(nc, ident[:])
+        nw = const.tile([P, N], BF16)
+        nc.scalar.dma_start(out=nw[:], in_=norm_w.partition_broadcast(P))
+
+        wc = {}
+        ws = {}
+        for b in range(2):
+            for g in range(2):
+                wc[(b, g)] = const.tile([P, 512], U32, name="wc%d%d" % (b, g), align_bytes=64)
+                ws[(b, g)] = const.tile([P, 512], U8, name="ws%d%d" % (b, g), align_bytes=64)
+
+        for b in range(2):
+            for jp in range(2):
+                srcs = []
+                for lp in range(5):
+                    raw = rawp.tile([P, 4096], BF16, tag="raw")
+                    nc.sync.dma_start(
+                        out=raw[:].rearrange("p (l c) -> p l c", l=2),
+                        in_=conv_w[2 * lp : 2 * lp + 2, 512 * b : 512 * b + 512, :].rearrange(
+                            "l (p j) h -> p l (j h)", j=4
+                        )[:, :, 2048 * jp : 2048 * jp + 2048],
+                    )
+                    if lp in S_PAIRS:
+                        for l in range(2):
+                            single = bigp.tile([P, 2048], F32, tag="big")
+                            nc.scalar.copy(
+                                out=split_write(single[:]),
+                                in_=perm_read(raw[:, 2048 * l : 2048 * l + 2048]),
+                            )
+                            srcs.append(single)
+                    else:
+                        pair = bigp.tile([P, 2048], F32, tag="big")
+                        nc.vector.tensor_tensor(
+                            out=split_write(pair[:]),
+                            in0=perm_read(raw[:, 0:2048]),
+                            in1=perm_read(raw[:, 2048:4096]),
+                            op=ALU.add,
+                        )
+                        srcs.append(pair)
+                for g in range(2):
+                    wgrp = grpp.tile([P, 1024], BF16, tag="wgrp", align_bytes=64)
+                    for j in range(2):
+                        wt = psum.tile([P, 512], F32, tag="bank")
+                        for t in range(4):
+                            col = (j * 8 + g * 4 + t) * 128
+                            for k, s in enumerate(srcs):
+                                nc.tensor.matmul(
+                                    out=wt[:, 128 * t : 128 * t + 128],
+                                    lhsT=s[:, col : col + 128],
+                                    rhs=ident[:],
+                                    start=(k == 0),
+                                    stop=(k == len(srcs) - 1),
+                                    is_transpose=True,
+                                )
+                        nc.scalar.copy(
+                            out=wgrp[:, 512 * j : 512 * j + 512].rearrange("p (n t) -> p n t", t=4),
+                            in_=wt[:].rearrange("p (t n) -> p n t", t=4),
+                        )
+                    nc.vector.quantize_mx(
+                        out=wc[(b, g)][:, 256 * jp : 256 * jp + 256].bitcast(FP8X4),
+                        scales=ws[(b, g)][:, 256 * jp : 256 * jp + 256],
+                        in_=wgrp[:],
+                    )
+
+        xc = []
+        xs = []
+        for a in range(4):
+            xraw = rawp.tile([P, 4096], BF16, tag="raw")
+            nc.sync.dma_start(
+                out=xraw[:],
+                in_=x_flat[512 * a : 512 * a + 512, :].rearrange("(p i) h -> p (i h)", i=4),
+            )
+            xw = xraw[:].bitcast(F32)
+            for i in range(4):
+                xt = psum.tile([P, 512], F32, tag="bank")
+                for c in range(4):
+                    nc.tensor.transpose(
+                        xt[:, 128 * c : 128 * c + 128],
+                        xw[:, 512 * i + 128 * c : 512 * i + 128 * c + 128],
+                        ident[:],
+                    )
+                xgrp = grpp.tile([P, 1024], BF16, tag="xgrp", align_bytes=64)
+                dst = xgrp[:].bitcast(F32).rearrange("p (g r u) -> p g r u", g=2, u=2)
+                src = xt[:].rearrange("p (g u r) -> p g r u", g=2, u=2)
+                if i % 2 == 0:
+                    nc.scalar.copy(out=dst, in_=src)
+                else:
+                    nc.vector.tensor_copy(out=dst, in_=src)
+                xcode = xcp.tile([P, 256], U32, tag="xc", align_bytes=64)
+                xscale = xcp.tile([P, 256], U8, tag="xs", align_bytes=64)
+                nc.vector.quantize_mx(out=xcode[:].bitcast(FP8X4), scales=xscale[:], in_=xgrp[:])
+                xc.append(xcode)
+                xs.append(xscale)
+
+        for a in range(4):
+            for ip in range(2):
+                osb = bigp.tile([P, 2048], F32, tag="big")
+                for i2 in range(2):
+                    m = 4 * a + 2 * ip + i2
+                    ss = small.tile([P, 2], F32, tag="ss")
+                    accs = []
+                    for b in range(2):
+                        acc = psum.tile([P, 512], F32, tag="bank")
+                        for g in range(2):
+                            nc.tensor.matmul_mx(
+                                out=acc[:],
+                                lhsT=xc[m][:, 128 * g : 128 * g + 128].bitcast(FP8X4),
+                                lhsT_scale=xs[m][:, 128 * g : 128 * g + 128],
+                                rhs=wc[(b, g)][:].bitcast(FP8X4),
+                                rhs_scale=ws[(b, g)][:],
+                                start=(g == 0),
+                                stop=(g == 1),
+                            )
+                        junk = junkp.tile([P, 512], BF16, tag="junk")
+                        nc.scalar.activation(
+                            out=junk[:], in_=acc[:], func=ACT.Square, accum_out=ss[:, b : b + 1]
+                        )
+                        accs.append(acc)
+                    tot = small.tile([P, 1], F32, tag="tot")
+                    nc.vector.scalar_tensor_tensor(
+                        out=tot[:],
+                        in0=ss[:, 0:1],
+                        scalar=EPS * L * L * H,
+                        in1=ss[:, 1:2],
+                        op0=ALU.add,
+                        op1=ALU.add,
+                    )
+                    root = small.tile([P, 1], F32, tag="root")
+                    nc.scalar.activation(out=root[:], in_=tot[:], func=ACT.Sqrt, scale=1.0 / H)
+                    rinv = small.tile([P, 1], F32, tag="rinv")
+                    nc.vector.reciprocal(out=rinv[:], in_=root[:])
+                    for b in range(2):
+                        lo = 1024 * i2 + 512 * b
+                        nc.vector.scalar_tensor_tensor(
+                            out=osb[:, lo : lo + 512].rearrange("t (p j) -> t p j", j=4),
+                            in0=accs[b][:].rearrange("t (j p) -> t p j", j=4),
+                            scalar=rinv[:, 0:1],
+                            in1=nw[:, 512 * b : 512 * b + 512].rearrange("t (p j) -> t p j", j=4),
+                            op0=ALU.mult,
+                            op1=ALU.mult,
+                        )
+                nc.sync.dma_start(
+                    out=out_flat[512 * a : 512 * a + 512, :].rearrange("(p i) n -> p (i n)", i=4)[
+                        :, 2048 * ip : 2048 * ip + 2048
+                    ],
+                    in_=osb[:],
+                )

@@ -51,6 +51,8 @@ def tile_conv2dlinalgrmsnorm_kernel(tc, hidden_states, conv_w, norm_w, out):
 
         ident = const.tile([P, P], F32)
         make_identity(nc, ident[:])
+        ident_bf = const.tile([P, P], BF16)
+        make_identity(nc, ident_bf[:])
         nw = const.tile([P, N], BF16)
         nc.scalar.dma_start(out=nw[:], in_=norm_w.partition_broadcast(P))
 
@@ -73,13 +75,13 @@ def tile_conv2dlinalgrmsnorm_kernel(tc, hidden_states, conv_w, norm_w, out):
                         )[:, :, 2048 * jp : 2048 * jp + 2048],
                     )
                     if lp in S_PAIRS:
-                        for l in range(2):
-                            single = bigp.tile([P, 2048], F32, tag="big")
-                            nc.scalar.copy(
-                                out=split_write(single[:]),
-                                in_=perm_read(raw[:, 2048 * l : 2048 * l + 2048]),
-                            )
-                            srcs.append(single)
+                        direct = raw
+                        single = bigp.tile([P, 2048], F32, tag="big")
+                        nc.scalar.copy(
+                            out=split_write(single[:]),
+                            in_=perm_read(raw[:, 2048:4096]),
+                        )
+                        srcs.append(single)
                     else:
                         pair = bigp.tile([P, 2048], F32, tag="big")
                         nc.vector.tensor_tensor(
@@ -95,14 +97,22 @@ def tile_conv2dlinalgrmsnorm_kernel(tc, hidden_states, conv_w, norm_w, out):
                         wt = psum.tile([P, 512], F32, tag="bank")
                         for t in range(4):
                             col = (j * 8 + g * 4 + t) * 128
+                            base = j * 1024 + g * 512 + (t // 2) * 256
+                            nc.tensor.matmul(
+                                out=wt[:, 128 * t : 128 * t + 128],
+                                lhsT=direct[:, base : base + 256].rearrange("p (q e) -> p e q", e=2)[:, t % 2, :],
+                                rhs=ident_bf[:],
+                                start=True,
+                                stop=False,
+                            )
                             for k, s in enumerate(srcs):
                                 nc.tensor.matmul(
                                     out=wt[:, 128 * t : 128 * t + 128],
                                     lhsT=s[:, col : col + 128],
                                     rhs=ident[:],
-                                    start=(k == 0),
+                                    start=False,
                                     stop=(k == len(srcs) - 1),
-                                    is_transpose=True,
+                                    is_transpose=(not (k == 0 and t % 2 == 0)),
                                 )
                         nc.scalar.copy(
                             out=wgrp[:, 512 * j : 512 * j + 512].rearrange("p (n t) -> p n t", t=4),

@@ -19,15 +19,16 @@ TOKENS = 2048
 EPS = 1e-06
 FLOPS = 2 * TOKENS * H * N
 
-S_PAIRS = (0,)
+LEAD = 4
+TILES = 16
 
 
-def perm_read(ap):
-    return ap.rearrange("p (c q e) -> p c e q", c=8, q=128, e=2)
+def perm_read(ap, c):
+    return ap.rearrange("p (c q e) -> p c e q", c=c, q=128, e=2)
 
 
-def split_write(ap):
-    return ap.rearrange("p (c e q) -> p c e q", c=8, q=128, e=2)
+def split_write(ap, c):
+    return ap.rearrange("p (c e q) -> p c e q", c=c, q=128, e=2)
 
 
 def tile_conv2dlinalgrmsnorm_kernel(tc, hidden_states, conv_w, norm_w, out):
@@ -37,24 +38,25 @@ def tile_conv2dlinalgrmsnorm_kernel(tc, hidden_states, conv_w, norm_w, out):
     with ExitStack() as ctx:
         const = ctx.enter_context(tc.tile_pool(name="const", bufs=1))
         rawp = ctx.enter_context(tc.tile_pool(name="rawp", bufs=8))
-        bigp = ctx.enter_context(tc.tile_pool(name="bigp", bufs=10))
+        bigp = ctx.enter_context(tc.tile_pool(name="bigp", bufs=6))
+        outp = ctx.enter_context(tc.tile_pool(name="outp", bufs=4))
         grpp = ctx.enter_context(tc.tile_pool(name="grpp", bufs=4))
         xcp = ctx.enter_context(tc.tile_pool(name="xcp", bufs=16))
         junkp = ctx.enter_context(tc.tile_pool(name="junkp", bufs=2))
         small = ctx.enter_context(tc.tile_pool(name="small", bufs=4))
         psum = ctx.enter_context(tc.psum_pool(name="psum", bufs=8))
+        ctx.enter_context(tc.manual_schedule())
 
+        nw = const.tile([P, N], BF16)
+        nc.scalar.dma_start(out=nw[:], in_=norm_w.partition_broadcast(P))
         warm_in = const.tile([P, 1], F32)
         nc.vector.memset(warm_in[:], 1.0)
         warm_out = const.tile([P, 1], F32)
         nc.scalar.activation(out=warm_out[:], in_=warm_in[:], func=ACT.Sqrt)
-
-        ident = const.tile([P, P], F32)
-        make_identity(nc, ident[:])
         ident_bf = const.tile([P, P], BF16)
         make_identity(nc, ident_bf[:])
-        nw = const.tile([P, N], BF16)
-        nc.scalar.dma_start(out=nw[:], in_=norm_w.partition_broadcast(P))
+        ident = const.tile([P, P], F32)
+        make_identity(nc, ident[:])
 
         wc = {}
         ws = {}
@@ -63,147 +65,249 @@ def tile_conv2dlinalgrmsnorm_kernel(tc, hidden_states, conv_w, norm_w, out):
                 wc[(b, g)] = const.tile([P, 512], U32, name="wc%d%d" % (b, g), align_bytes=64)
                 ws[(b, g)] = const.tile([P, 512], U8, name="ws%d%d" % (b, g), align_bytes=64)
 
-        for b in range(2):
-            for jp in range(2):
-                srcs = []
-                for lp in range(5):
-                    raw = rawp.tile([P, 4096], BF16, tag="raw")
-                    nc.sync.dma_start(
-                        out=raw[:].rearrange("p (l c) -> p l c", l=2),
-                        in_=conv_w[2 * lp : 2 * lp + 2, 512 * b : 512 * b + 512, :].rearrange(
-                            "l (p j) h -> p l (j h)", j=4
-                        )[:, :, 2048 * jp : 2048 * jp + 2048],
+        def w_run(c, k, src, direct, banks):
+            for beta in range(4):
+                g, j = divmod(beta, 2)
+                if k < 4:
+                    base = j * 1024 + g * 512 + (k // 2) * 256
+                    nc.tensor.matmul(
+                        out=banks[beta][:, 128 * k : 128 * k + 128],
+                        lhsT=direct[:, base : base + 256].rearrange("p (q e) -> p e q", e=2)[:, k % 2, :],
+                        rhs=ident_bf[:],
+                        start=(k == 0),
+                        stop=False,
                     )
-                    if lp in S_PAIRS:
-                        direct = raw
-                        single = bigp.tile([P, 2048], F32, tag="big")
-                        nc.scalar.copy(
-                            out=split_write(single[:]),
-                            in_=perm_read(raw[:, 2048:4096]),
-                        )
-                        srcs.append(single)
+                for t in range(4):
+                    col = (j * 8 + g * 4 + t) * 128
+                    if k < 4:
+                        plain = t == 2 and beta % 2 == 0
                     else:
-                        pair = bigp.tile([P, 2048], F32, tag="big")
-                        nc.vector.tensor_tensor(
-                            out=split_write(pair[:]),
-                            in0=perm_read(raw[:, 0:2048]),
-                            in1=perm_read(raw[:, 2048:4096]),
-                            op=ALU.add,
-                        )
-                        srcs.append(pair)
-                for g in range(2):
-                    wgrp = grpp.tile([P, 1024], BF16, tag="wgrp", align_bytes=64)
-                    for j in range(2):
-                        wt = psum.tile([P, 512], F32, tag="bank")
-                        for t in range(4):
-                            col = (j * 8 + g * 4 + t) * 128
-                            base = j * 1024 + g * 512 + (t // 2) * 256
-                            nc.tensor.matmul(
-                                out=wt[:, 128 * t : 128 * t + 128],
-                                lhsT=direct[:, base : base + 256].rearrange("p (q e) -> p e q", e=2)[:, t % 2, :],
-                                rhs=ident_bf[:],
-                                start=True,
-                                stop=False,
-                            )
-                            for k, s in enumerate(srcs):
-                                nc.tensor.matmul(
-                                    out=wt[:, 128 * t : 128 * t + 128],
-                                    lhsT=s[:, col : col + 128],
-                                    rhs=ident[:],
-                                    start=False,
-                                    stop=(k == len(srcs) - 1),
-                                    is_transpose=(not (k == 0 and t % 2 == 0)),
-                                )
-                        nc.scalar.copy(
-                            out=wgrp[:, 512 * j : 512 * j + 512].rearrange("p (n t) -> p n t", t=4),
-                            in_=wt[:].rearrange("p (t n) -> p n t", t=4),
-                        )
-                    nc.vector.quantize_mx(
-                        out=wc[(b, g)][:, 256 * jp : 256 * jp + 256].bitcast(FP8X4),
-                        scales=ws[(b, g)][:, 256 * jp : 256 * jp + 256],
-                        in_=wgrp[:],
+                        plain = t == 1 and beta == 1 and c < 3
+                    nc.tensor.matmul(
+                        out=banks[beta][:, 128 * t : 128 * t + 128],
+                        lhsT=src[:, col : col + 128],
+                        rhs=ident[:],
+                        start=False,
+                        stop=(k == 4 and t == 3),
+                        is_transpose=(not plain),
                     )
 
-        xc = []
-        xs = []
+        def w_evac(banks, groups, beta):
+            g, j = divmod(beta, 2)
+            nc.scalar.copy(
+                out=groups[g][:, 512 * j : 512 * j + 512].rearrange("p (n t) -> p n t", t=4),
+                in_=banks[beta][:].rearrange("p (t n) -> p n t", t=4),
+            )
+
+        def w_quant(c, groups, g):
+            b, jp = divmod(c, 2)
+            nc.vector.quantize_mx(
+                out=wc[(b, g)][:, 256 * jp : 256 * jp + 256].bitcast(FP8X4),
+                scales=ws[(b, g)][:, 256 * jp : 256 * jp + 256],
+                in_=groups[g][:],
+            )
+
+        prev = None
+        for c in range(4):
+            b, jp = divmod(c, 2)
+            raws = []
+            for lp in range(5):
+                raw = rawp.tile([P, 4096], BF16, tag="raw", name="raw%d_%d" % (c, lp))
+                nc.sync.dma_start(
+                    out=raw[:].rearrange("p (l c) -> p l c", l=2),
+                    in_=conv_w[2 * lp : 2 * lp + 2, 512 * b : 512 * b + 512, :].rearrange(
+                        "l (p j) h -> p l (j h)", j=4
+                    )[:, :, 2048 * jp : 2048 * jp + 2048],
+                )
+                raws.append(raw)
+            banks = [psum.tile([P, 512], F32, tag="bank", name="wb%d_%d" % (c, beta)) for beta in range(4)]
+            groups = [
+                grpp.tile([P, 1024], BF16, tag="wgrp", name="wg%d_%d" % (c, g), align_bytes=64) for g in range(2)
+            ]
+            single = bigp.tile([P, 2048], F32, tag="big", name="single%d" % c)
+            nc.scalar.copy(out=split_write(single[:], 8), in_=perm_read(raws[0][:, 2048:4096], 8))
+            if prev is not None:
+                for beta in range(4):
+                    w_evac(prev[0], prev[1], beta)
+            w_run(c, 0, single, raws[0], banks)
+            for lp in range(1, 5):
+                pair = bigp.tile([P, 2048], F32, tag="big", name="pair%d_%d" % (c, lp))
+                if c == 3 and lp == 4:
+                    for beta in range(4):
+                        g, j = divmod(beta, 2)
+                        lo = j * 1024 + g * 512
+                        nc.vector.tensor_tensor(
+                            out=split_write(pair[:, lo : lo + 512], 2),
+                            in0=perm_read(raws[lp][:, lo : lo + 512], 2),
+                            in1=perm_read(raws[lp][:, 2048 + lo : 2048 + lo + 512], 2),
+                            op=ALU.add,
+                        )
+                else:
+                    nc.vector.tensor_tensor(
+                        out=split_write(pair[:], 8),
+                        in0=perm_read(raws[lp][:, 0:2048], 8),
+                        in1=perm_read(raws[lp][:, 2048:4096], 8),
+                        op=ALU.add,
+                    )
+                if lp == 1 and prev is not None:
+                    w_quant(c - 1, prev[1], 0)
+                    w_quant(c - 1, prev[1], 1)
+                w_run(c, lp, pair, raws[0], banks)
+            prev = (banks, groups)
+        for beta in range(4):
+            w_evac(prev[0], prev[1], beta)
+            if beta % 2 == 1:
+                w_quant(3, prev[1], beta // 2)
+
+        xraws = []
         for a in range(4):
-            xraw = rawp.tile([P, 4096], BF16, tag="raw")
+            xraw = rawp.tile([P, 4096], BF16, tag="raw", name="xraw%d" % a)
             nc.sync.dma_start(
                 out=xraw[:],
                 in_=x_flat[512 * a : 512 * a + 512, :].rearrange("(p i) h -> p (i h)", i=4),
             )
-            xw = xraw[:].bitcast(F32)
-            for i in range(4):
-                xt = psum.tile([P, 512], F32, tag="bank")
-                for c in range(4):
-                    nc.tensor.transpose(
-                        xt[:, 128 * c : 128 * c + 128],
-                        xw[:, 512 * i + 128 * c : 512 * i + 128 * c + 128],
-                        ident[:],
-                    )
-                xgrp = grpp.tile([P, 1024], BF16, tag="xgrp", align_bytes=64)
-                dst = xgrp[:].bitcast(F32).rearrange("p (g r u) -> p g r u", g=2, u=2)
-                src = xt[:].rearrange("p (g u r) -> p g r u", g=2, u=2)
-                if i % 2 == 0:
-                    nc.scalar.copy(out=dst, in_=src)
-                else:
-                    nc.vector.tensor_copy(out=dst, in_=src)
-                xcode = xcp.tile([P, 256], U32, tag="xc", align_bytes=64)
-                xscale = xcp.tile([P, 256], U8, tag="xs", align_bytes=64)
-                nc.vector.quantize_mx(out=xcode[:].bitcast(FP8X4), scales=xscale[:], in_=xgrp[:])
-                xc.append(xcode)
-                xs.append(xscale)
+            xraws.append(xraw)
 
-        for a in range(4):
-            for ip in range(2):
-                osb = bigp.tile([P, 2048], F32, tag="big")
-                for i2 in range(2):
-                    m = 4 * a + 2 * ip + i2
-                    ss = small.tile([P, 2], F32, tag="ss")
-                    accs = []
-                    for b in range(2):
-                        acc = psum.tile([P, 512], F32, tag="bank")
-                        for g in range(2):
-                            nc.tensor.matmul_mx(
-                                out=acc[:],
-                                lhsT=xc[m][:, 128 * g : 128 * g + 128].bitcast(FP8X4),
-                                lhsT_scale=xs[m][:, 128 * g : 128 * g + 128],
-                                rhs=wc[(b, g)][:].bitcast(FP8X4),
-                                rhs_scale=ws[(b, g)][:],
-                                start=(g == 0),
-                                stop=(g == 1),
-                            )
-                        junk = junkp.tile([P, 512], BF16, tag="junk")
-                        nc.scalar.activation(
-                            out=junk[:], in_=acc[:], func=ACT.Square, accum_out=ss[:, b : b + 1]
-                        )
-                        accs.append(acc)
-                    tot = small.tile([P, 1], F32, tag="tot")
-                    nc.vector.scalar_tensor_tensor(
-                        out=tot[:],
-                        in0=ss[:, 0:1],
-                        scalar=EPS * L * L * H,
-                        in1=ss[:, 1:2],
-                        op0=ALU.add,
-                        op1=ALU.add,
-                    )
-                    root = small.tile([P, 1], F32, tag="root")
-                    nc.scalar.activation(out=root[:], in_=tot[:], func=ACT.Sqrt, scale=1.0 / H)
-                    rinv = small.tile([P, 1], F32, tag="rinv")
-                    nc.vector.reciprocal(out=rinv[:], in_=root[:])
-                    for b in range(2):
-                        lo = 1024 * i2 + 512 * b
-                        nc.vector.scalar_tensor_tensor(
-                            out=osb[:, lo : lo + 512].rearrange("t (p j) -> t p j", j=4),
-                            in0=accs[b][:].rearrange("t (j p) -> t p j", j=4),
-                            scalar=rinv[:, 0:1],
-                            in1=nw[:, 512 * b : 512 * b + 512].rearrange("t (p j) -> t p j", j=4),
-                            op0=ALU.mult,
-                            op1=ALU.mult,
-                        )
-                nc.sync.dma_start(
-                    out=out_flat[512 * a : 512 * a + 512, :].rearrange("(p i) n -> p (i n)", i=4)[
-                        :, 2048 * ip : 2048 * ip + 2048
-                    ],
-                    in_=osb[:],
+        xt = {}
+        xg = {}
+        xc = {}
+        xs = {}
+        acc = {}
+        ss = {}
+        tot = {}
+        root = {}
+        rinv = {}
+        osb = {}
+
+        def x_t(m):
+            a, i = divmod(m, 4)
+            xw = xraws[a][:].bitcast(F32)
+            xt[m] = psum.tile([P, 512], F32, tag="bank", name="xt%d" % m)
+            for cc in range(4):
+                nc.tensor.transpose(
+                    xt[m][:, 128 * cc : 128 * cc + 128],
+                    xw[:, 512 * i + 128 * cc : 512 * i + 128 * cc + 128],
+                    ident[:],
                 )
+
+        def x_evac(m):
+            xg[m] = grpp.tile([P, 1024], BF16, tag="xgrp", name="xg%d" % m, align_bytes=64)
+            dst = xg[m][:].bitcast(F32).rearrange("p (g r u) -> p g r u", g=2, u=2)
+            src = xt[m][:].rearrange("p (g u r) -> p g r u", g=2, u=2)
+            if m % 4 == 3:
+                nc.vector.tensor_copy(out=dst, in_=src)
+            else:
+                nc.scalar.copy(out=dst, in_=src)
+
+        def x_quant(m):
+            xc[m] = xcp.tile([P, 256], U32, tag="xc", name="xc%d" % m, align_bytes=64)
+            xs[m] = xcp.tile([P, 256], U8, tag="xs", name="xs%d" % m, align_bytes=64)
+            nc.vector.quantize_mx(out=xc[m][:].bitcast(FP8X4), scales=xs[m][:], in_=xg[m][:])
+
+        def mx(m):
+            for b in range(2):
+                acc[(m, b)] = psum.tile([P, 512], F32, tag="bank", name="acc%d_%d" % (m, b))
+                for g in range(2):
+                    nc.tensor.matmul_mx(
+                        out=acc[(m, b)][:],
+                        lhsT=xc[m][:, 128 * g : 128 * g + 128].bitcast(FP8X4),
+                        lhsT_scale=xs[m][:, 128 * g : 128 * g + 128],
+                        rhs=wc[(b, g)][:].bitcast(FP8X4),
+                        rhs_scale=ws[(b, g)][:],
+                        start=(g == 0),
+                        stop=(g == 1),
+                    )
+
+        def sumsq(m, b):
+            if b == 0:
+                ss[m] = small.tile([P, 2], F32, tag="ss", name="ss%d" % m)
+            junk = junkp.tile([P, 512], BF16, tag="junk", name="junk%d_%d" % (m, b))
+            nc.scalar.activation(
+                out=junk[:], in_=acc[(m, b)][:], func=ACT.Square, scale=1.0 / 32.0, accum_out=ss[m][:, b : b + 1]
+            )
+
+        def total(m):
+            tot[m] = small.tile([P, 1], F32, tag="tot", name="tot%d" % m)
+            nc.vector.scalar_tensor_tensor(
+                out=tot[m][:],
+                in0=ss[m][:, 0:1],
+                scalar=EPS * L * L,
+                in1=ss[m][:, 1:2],
+                op0=ALU.add,
+                op1=ALU.add,
+            )
+
+        def sqrt(m):
+            root[m] = small.tile([P, 1], F32, tag="root", name="root%d" % m)
+            nc.scalar.activation(out=root[m][:], in_=tot[m][:], func=ACT.Sqrt)
+
+        def recip(m):
+            rinv[m] = small.tile([P, 1], F32, tag="rinv", name="rinv%d" % m)
+            nc.vector.reciprocal(out=rinv[m][:], in_=root[m][:])
+
+        def final(m, b):
+            if b == 0:
+                osb[m] = outp.tile([P, 1024], F32, tag="osb", name="osb%d" % m)
+            nc.vector.scalar_tensor_tensor(
+                out=osb[m][:, 512 * b : 512 * b + 512].rearrange("t (p j) -> t p j", j=4),
+                in0=acc[(m, b)][:].rearrange("t (j p) -> t p j", j=4),
+                scalar=rinv[m][:, 0:1],
+                in1=nw[:, 512 * b : 512 * b + 512].rearrange("t (p j) -> t p j", j=4),
+                op0=ALU.mult,
+                op1=ALU.mult,
+            )
+
+        def store(m, lo, hi):
+            a, i = divmod(m, 4)
+            nc.sync.dma_start(
+                out=out_flat[512 * a : 512 * a + 512, :].rearrange("(p i) n -> p i n", i=4)[:, i, lo:hi],
+                in_=osb[m][:, lo:hi],
+            )
+
+        for k in range(LEAD):
+            x_t(k)
+        for k in range(LEAD):
+            x_evac(k)
+            if k >= 1:
+                x_quant(k - 1)
+        x_quant(LEAD - 1)
+        mx(0)
+        mx(1)
+        nxt = LEAD
+        if nxt < TILES:
+            x_t(nxt)
+            x_t(nxt + 1)
+        pend_evac = [nxt, nxt + 1] if nxt < TILES else []
+        pend_quant = []
+        nxt += 2
+        for m in range(TILES + 1):
+            if m < TILES:
+                sumsq(m, 0)
+            if m >= 1:
+                sqrt(m - 1)
+                recip(m - 1)
+                final(m - 1, 0)
+                if m == TILES:
+                    store(m - 1, 0, 512)
+            if m < TILES:
+                sumsq(m, 1)
+                total(m)
+            if m >= 1:
+                final(m - 1, 1)
+                if m == TILES:
+                    store(m - 1, 512, 1024)
+                else:
+                    store(m - 1, 0, 1024)
+            if pend_quant:
+                x_quant(pend_quant.pop(0))
+            if pend_evac:
+                k = pend_evac.pop(0)
+                x_evac(k)
+                pend_quant.append(k)
+            if m + 2 < TILES:
+                mx(m + 2)
+                if m % 2 == 1 and nxt < TILES:
+                    x_t(nxt)
+                    x_t(nxt + 1)
+                    pend_evac.extend([nxt, nxt + 1])
+                    nxt += 2

@@ -21,6 +21,7 @@ FLOPS = 2 * TOKENS * H * N
 
 LEAD = 4
 TILES = 16
+PLAIN_F32 = (1, 2, 2, 1, 2)
 
 
 def perm_read(ap, c):
@@ -66,9 +67,9 @@ def tile_conv2dlinalgrmsnorm_kernel(tc, hidden_states, conv_w, norm_w, out):
                 ws[(b, g)] = const.tile([P, 512], U8, name="ws%d%d" % (b, g), align_bytes=64)
 
         def w_run(c, k, src, direct, banks):
-            for beta in range(4):
-                g, j = divmod(beta, 2)
-                if k < 4:
+            if k < 4:
+                for beta in range(4):
+                    g, j = divmod(beta, 2)
                     base = j * 1024 + g * 512 + (k // 2) * 256
                     nc.tensor.matmul(
                         out=banks[beta][:, 128 * k : 128 * k + 128],
@@ -77,19 +78,18 @@ def tile_conv2dlinalgrmsnorm_kernel(tc, hidden_states, conv_w, norm_w, out):
                         start=(k == 0),
                         stop=False,
                     )
+            n_plain = 0 if (c == 3 and k == 4) else PLAIN_F32[k]
+            for beta in range(4):
+                g, j = divmod(beta, 2)
                 for t in range(4):
                     col = (j * 8 + g * 4 + t) * 128
-                    if k < 4:
-                        plain = t == 2 and beta % 2 == 0
-                    else:
-                        plain = t == 1 and beta == 1 and c < 3
                     nc.tensor.matmul(
                         out=banks[beta][:, 128 * t : 128 * t + 128],
                         lhsT=src[:, col : col + 128],
                         rhs=ident[:],
                         start=False,
                         stop=(k == 4 and t == 3),
-                        is_transpose=(not plain),
+                        is_transpose=(4 * beta + t >= n_plain),
                     )
 
         def w_evac(banks, groups, beta):

@@ -19,7 +19,7 @@ TOKENS = 2048
 EPS = 1e-06
 FLOPS = 2 * TOKENS * H * N
 
-LEAD = 4
+LEAD = 8
 TILES = 16
 PLAIN_F32 = (1, 2, 2, 1, 2)
 
@@ -50,10 +50,8 @@ def tile_conv2dlinalgrmsnorm_kernel(tc, hidden_states, conv_w, norm_w, out):
 
         nw = const.tile([P, N], BF16)
         nc.scalar.dma_start(out=nw[:], in_=norm_w.partition_broadcast(P))
-        warm_in = const.tile([P, 1], F32)
-        nc.vector.memset(warm_in[:], 1.0)
-        warm_out = const.tile([P, 1], F32)
-        nc.scalar.activation(out=warm_out[:], in_=warm_in[:], func=ACT.Sqrt)
+        neg_half = const.tile([P, 1], F32)
+        nc.vector.memset(neg_half[:], -0.5)
         ident_bf = const.tile([P, P], BF16)
         make_identity(nc, ident_bf[:])
         ident = const.tile([P, P], F32)
@@ -175,7 +173,6 @@ def tile_conv2dlinalgrmsnorm_kernel(tc, hidden_states, conv_w, norm_w, out):
         acc = {}
         ss = {}
         tot = {}
-        root = {}
         rinv = {}
         osb = {}
 
@@ -194,7 +191,7 @@ def tile_conv2dlinalgrmsnorm_kernel(tc, hidden_states, conv_w, norm_w, out):
             xg[m] = grpp.tile([P, 1024], BF16, tag="xgrp", name="xg%d" % m, align_bytes=64)
             dst = xg[m][:].bitcast(F32).rearrange("p (g r u) -> p g r u", g=2, u=2)
             src = xt[m][:].rearrange("p (g u r) -> p g r u", g=2, u=2)
-            if m % 4 == 3:
+            if m % 3 == 2:
                 nc.vector.tensor_copy(out=dst, in_=src)
             else:
                 nc.scalar.copy(out=dst, in_=src)
@@ -226,24 +223,18 @@ def tile_conv2dlinalgrmsnorm_kernel(tc, hidden_states, conv_w, norm_w, out):
                 out=junk[:], in_=acc[(m, b)][:], func=ACT.Square, scale=1.0 / 32.0, accum_out=ss[m][:, b : b + 1]
             )
 
-        def total(m):
+        def chain(m):
             tot[m] = small.tile([P, 1], F32, tag="tot", name="tot%d" % m)
-            nc.vector.scalar_tensor_tensor(
+            nc.gpsimd.tensor_scalar(
                 out=tot[m][:],
                 in0=ss[m][:, 0:1],
-                scalar=EPS * L * L,
-                in1=ss[m][:, 1:2],
+                scalar1=ss[m][:, 1:2],
+                scalar2=EPS * L * L,
                 op0=ALU.add,
                 op1=ALU.add,
             )
-
-        def sqrt(m):
-            root[m] = small.tile([P, 1], F32, tag="root", name="root%d" % m)
-            nc.scalar.activation(out=root[m][:], in_=tot[m][:], func=ACT.Sqrt)
-
-        def recip(m):
             rinv[m] = small.tile([P, 1], F32, tag="rinv", name="rinv%d" % m)
-            nc.vector.reciprocal(out=rinv[m][:], in_=root[m][:])
+            nc.gpsimd.tensor_tensor(out=rinv[m][:], in0=tot[m][:], in1=neg_half[:], op=ALU.pow)
 
         def final(m, b):
             if b == 0:
@@ -283,16 +274,12 @@ def tile_conv2dlinalgrmsnorm_kernel(tc, hidden_states, conv_w, norm_w, out):
         for m in range(TILES + 1):
             if m < TILES:
                 sumsq(m, 0)
+                sumsq(m, 1)
+                chain(m)
             if m >= 1:
-                sqrt(m - 1)
-                recip(m - 1)
                 final(m - 1, 0)
                 if m == TILES:
                     store(m - 1, 0, 512)
-            if m < TILES:
-                sumsq(m, 1)
-                total(m)
-            if m >= 1:
                 final(m - 1, 1)
                 if m == TILES:
                     store(m - 1, 512, 1024)

@@ -21,7 +21,7 @@ FLOPS = 2 * TOKENS * H * N
 
 LEAD = 8
 TILES = 16
-PLAIN_F32 = (1, 2, 2, 1, 2)
+PLAIN_F32 = (1, 2, 2, 1, 1)
 
 
 def perm_read(ap, c):
@@ -48,8 +48,12 @@ def tile_conv2dlinalgrmsnorm_kernel(tc, hidden_states, conv_w, norm_w, out):
         psum = ctx.enter_context(tc.psum_pool(name="psum", bufs=8))
         ctx.enter_context(tc.manual_schedule())
 
+        nw_row = const.tile([P, N], BF16)
+        nc.vector.memset(nw_row[:], 0.0)
+        nc.scalar.dma_start(out=nw_row[0:1, :], in_=norm_w.rearrange("(o n) -> o n", o=1))
+        ones = const.tile([P, P], BF16)
+        nc.vector.memset(ones[:], 1.0)
         nw = const.tile([P, N], BF16)
-        nc.scalar.dma_start(out=nw[:], in_=norm_w.partition_broadcast(P))
         neg_half = const.tile([P, 1], F32)
         nc.vector.memset(neg_half[:], -0.5)
         ident_bf = const.tile([P, P], BF16)
@@ -128,6 +132,13 @@ def tile_conv2dlinalgrmsnorm_kernel(tc, hidden_states, conv_w, norm_w, out):
                 for beta in range(4):
                     w_evac(prev[0], prev[1], beta)
             w_run(c, 0, single, raws[0], banks)
+            if c == 0:
+                for b2 in range(2):
+                    spread = psum.tile([P, 512], F32, tag="bank", name="spread%d" % b2)
+                    nc.tensor.matmul(
+                        out=spread[:], lhsT=ones[:], rhs=nw_row[:, 512 * b2 : 512 * b2 + 512], start=True, stop=True
+                    )
+                    nc.scalar.copy(out=nw[:, 512 * b2 : 512 * b2 + 512], in_=spread[:])
             for lp in range(1, 5):
                 pair = bigp.tile([P, 2048], F32, tag="big", name="pair%d_%d" % (c, lp))
                 if c == 3 and lp == 4:

@@ -38,8 +38,8 @@ def tile_conv2dlinalgrmsnorm_kernel(tc, hidden_states, conv_w, norm_w, out):
     out_flat = out.flatten_outer_dims()
     with ExitStack() as ctx:
         const = ctx.enter_context(tc.tile_pool(name="const", bufs=1))
-        rawp = ctx.enter_context(tc.tile_pool(name="rawp", bufs=8))
-        bigp = ctx.enter_context(tc.tile_pool(name="bigp", bufs=6))
+        rawp = ctx.enter_context(tc.tile_pool(name="rawp", bufs=12))
+        bigp = ctx.enter_context(tc.tile_pool(name="bigp", bufs=8))
         outp = ctx.enter_context(tc.tile_pool(name="outp", bufs=4))
         grpp = ctx.enter_context(tc.tile_pool(name="grpp", bufs=4))
         xcp = ctx.enter_context(tc.tile_pool(name="xcp", bufs=16))

@@ -21,7 +21,7 @@ FLOPS = 2 * TOKENS * H * N
 
 LEAD = 8
 TILES = 16
-PLAIN_F32 = (1, 2, 2, 1, 1)
+PLAIN_F32 = (0, 0, 0, 0, 0)
 
 
 def perm_read(ap, c):
@@ -38,8 +38,8 @@ def tile_conv2dlinalgrmsnorm_kernel(tc, hidden_states, conv_w, norm_w, out):
     out_flat = out.flatten_outer_dims()
     with ExitStack() as ctx:
         const = ctx.enter_context(tc.tile_pool(name="const", bufs=1))
-        rawp = ctx.enter_context(tc.tile_pool(name="rawp", bufs=12))
-        bigp = ctx.enter_context(tc.tile_pool(name="bigp", bufs=8))
+        rawp = ctx.enter_context(tc.tile_pool(name="rawp", bufs=8))
+        bigp = ctx.enter_context(tc.tile_pool(name="bigp", bufs=6))
         outp = ctx.enter_context(tc.tile_pool(name="outp", bufs=4))
         grpp = ctx.enter_context(tc.tile_pool(name="grpp", bufs=4))
         xcp = ctx.enter_context(tc.tile_pool(name="xcp", bufs=16))

@@ -19,7 +19,7 @@ TOKENS = 2048
 EPS = 1e-06
 FLOPS = 2 * TOKENS * H * N
 
-LEAD = 8
+LEAD = 4
 TILES = 16
 PLAIN_F32 = (0, 0, 0, 0, 0)
 
@@ -50,7 +50,7 @@ def tile_conv2dlinalgrmsnorm_kernel(tc, hidden_states, conv_w, norm_w, out):
 
         nw_row = const.tile([P, N], BF16)
         nc.vector.memset(nw_row[:], 0.0)
-        nc.scalar.dma_start(out=nw_row[0:1, :], in_=norm_w.rearrange("(o n) -> o n", o=1))
+        nc.sync.dma_start(out=nw_row[0:1, :], in_=norm_w.rearrange("(o n) -> o n", o=1))
         ones = const.tile([P, P], BF16)
         nc.vector.memset(ones[:], 1.0)
         nw = const.tile([P, N], BF16)
@@ -108,6 +108,57 @@ def tile_conv2dlinalgrmsnorm_kernel(tc, hidden_states, conv_w, norm_w, out):
                 scales=ws[(b, g)][:, 256 * jp : 256 * jp + 256],
                 in_=groups[g][:],
             )
+
+        xraws = []
+        for a in range(4):
+            xraw = rawp.tile([P, 4096], BF16, tag="raw", name="xraw%d" % a)
+            nc.sync.dma_start(
+                out=xraw[:],
+                in_=x_flat[512 * a : 512 * a + 512, :].rearrange("(p i) h -> p (i h)", i=4),
+            )
+            xraws.append(xraw)
+
+        xt = {}
+        xg = {}
+        xc = {}
+        xs = {}
+        acc = {}
+        ss = {}
+        tot = {}
+        rinv = {}
+        osb = {}
+
+        def x_t(m):
+            a, i = divmod(m, 4)
+            xw = xraws[a][:].bitcast(F32)
+            xt[m] = psum.tile([P, 512], F32, tag="bank", name="xt%d" % m)
+            for cc in range(4):
+                nc.tensor.transpose(
+                    xt[m][:, 128 * cc : 128 * cc + 128],
+                    xw[:, 512 * i + 128 * cc : 512 * i + 128 * cc + 128],
+                    ident[:],
+                )
+
+        def x_evac(m):
+            xg[m] = grpp.tile([P, 1024], BF16, tag="xgrp", name="xg%d" % m, align_bytes=64)
+            dst = xg[m][:].bitcast(F32).rearrange("p (g r u) -> p g r u", g=2, u=2)
+            src = xt[m][:].rearrange("p (g u r) -> p g r u", g=2, u=2)
+            if m % 3 == 2:
+                nc.vector.tensor_copy(out=dst, in_=src)
+            else:
+                nc.scalar.copy(out=dst, in_=src)
+
+        def x_quant(m):
+            xc[m] = xcp.tile([P, 256], U32, tag="xc", name="xc%d" % m, align_bytes=64)
+            xs[m] = xcp.tile([P, 256], U8, tag="xs", name="xs%d" % m, align_bytes=64)
+            nc.vector.quantize_mx(out=xc[m][:].bitcast(FP8X4), scales=xs[m][:], in_=xg[m][:])
+
+        for k in range(TILES):
+            x_t(k)
+            x_evac(k)
+            if k >= 1:
+                x_quant(k - 1)
+        x_quant(TILES - 1)
 
         prev = None
         for c in range(4):
@@ -168,50 +219,6 @@ def tile_conv2dlinalgrmsnorm_kernel(tc, hidden_states, conv_w, norm_w, out):
             if beta % 2 == 1:
                 w_quant(3, prev[1], beta // 2)
 
-        xraws = []
-        for a in range(4):
-            xraw = rawp.tile([P, 4096], BF16, tag="raw", name="xraw%d" % a)
-            nc.sync.dma_start(
-                out=xraw[:],
-                in_=x_flat[512 * a : 512 * a + 512, :].rearrange("(p i) h -> p (i h)", i=4),
-            )
-            xraws.append(xraw)
-
-        xt = {}
-        xg = {}
-        xc = {}
-        xs = {}
-        acc = {}
-        ss = {}
-        tot = {}
-        rinv = {}
-        osb = {}
-
-        def x_t(m):
-            a, i = divmod(m, 4)
-            xw = xraws[a][:].bitcast(F32)
-            xt[m] = psum.tile([P, 512], F32, tag="bank", name="xt%d" % m)
-            for cc in range(4):
-                nc.tensor.transpose(
-                    xt[m][:, 128 * cc : 128 * cc + 128],
-                    xw[:, 512 * i + 128 * cc : 512 * i + 128 * cc + 128],
-                    ident[:],
-                )
-
-        def x_evac(m):
-            xg[m] = grpp.tile([P, 1024], BF16, tag="xgrp", name="xg%d" % m, align_bytes=64)
-            dst = xg[m][:].bitcast(F32).rearrange("p (g r u) -> p g r u", g=2, u=2)
-            src = xt[m][:].rearrange("p (g u r) -> p g r u", g=2, u=2)
-            if m % 3 == 2:
-                nc.vector.tensor_copy(out=dst, in_=src)
-            else:
-                nc.scalar.copy(out=dst, in_=src)
-
-        def x_quant(m):
-            xc[m] = xcp.tile([P, 256], U32, tag="xc", name="xc%d" % m, align_bytes=64)
-            xs[m] = xcp.tile([P, 256], U8, tag="xs", name="xs%d" % m, align_bytes=64)
-            nc.vector.quantize_mx(out=xc[m][:].bitcast(FP8X4), scales=xs[m][:], in_=xg[m][:])
-
         def mx(m):
             for b in range(2):
                 acc[(m, b)] = psum.tile([P, 512], F32, tag="bank", name="acc%d_%d" % (m, b))
@@ -266,22 +273,8 @@ def tile_conv2dlinalgrmsnorm_kernel(tc, hidden_states, conv_w, norm_w, out):
                 in_=osb[m][:, lo:hi],
             )
 
-        for k in range(LEAD):
-            x_t(k)
-        for k in range(LEAD):
-            x_evac(k)
-            if k >= 1:
-                x_quant(k - 1)
-        x_quant(LEAD - 1)
-        mx(0)
-        mx(1)
-        nxt = LEAD
-        if nxt < TILES:
-            x_t(nxt)
-            x_t(nxt + 1)
-        pend_evac = [nxt, nxt + 1] if nxt < TILES else []
-        pend_quant = []
-        nxt += 2
+        for m in range(LEAD):
+            mx(m)
         for m in range(TILES + 1):
             if m < TILES:
                 sumsq(m, 0)
@@ -296,16 +289,5 @@ def tile_conv2dlinalgrmsnorm_kernel(tc, hidden_states, conv_w, norm_w, out):
                     store(m - 1, 512, 1024)
                 else:
                     store(m - 1, 0, 1024)
-            if pend_quant:
-                x_quant(pend_quant.pop(0))
-            if pend_evac:
-                k = pend_evac.pop(0)
-                x_evac(k)
-                pend_quant.append(k)
-            if m + 2 < TILES:
-                mx(m + 2)
-                if m % 2 == 1 and nxt < TILES:
-                    x_t(nxt)
-                    x_t(nxt + 1)
-                    pend_evac.extend([nxt, nxt + 1])
-                    nxt += 2
+            if m >= 1 and m - 1 + LEAD < TILES:
+                mx(m - 1 + LEAD)

@@ -54,8 +54,9 @@ def tile_conv2dlinalgrmsnorm_kernel(tc, hidden_states, conv_w, norm_w, out):
         ones = const.tile([P, P], BF16)
         nc.vector.memset(ones[:], 1.0)
         nw = const.tile([P, N], BF16)
-        neg_half = const.tile([P, 1], F32)
-        nc.vector.memset(neg_half[:], -0.5)
+        warm = const.tile([P, 1], F32)
+        nc.vector.memset(warm[:], 1.0)
+        nc.scalar.activation(out=warm[:], in_=warm[:], func=ACT.Abs_reciprocal_sqrt)
         ident_bf = const.tile([P, P], BF16)
         make_identity(nc, ident_bf[:])
         ident = const.tile([P, P], F32)
@@ -241,9 +242,9 @@ def tile_conv2dlinalgrmsnorm_kernel(tc, hidden_states, conv_w, norm_w, out):
                 out=junk[:], in_=acc[(m, b)][:], func=ACT.Square, scale=1.0 / 32.0, accum_out=ss[m][:, b : b + 1]
             )
 
-        def chain(m):
+        def total(m):
             tot[m] = small.tile([P, 1], F32, tag="tot", name="tot%d" % m)
-            nc.gpsimd.tensor_scalar(
+            nc.vector.tensor_scalar(
                 out=tot[m][:],
                 in0=ss[m][:, 0:1],
                 scalar1=ss[m][:, 1:2],
@@ -251,8 +252,10 @@ def tile_conv2dlinalgrmsnorm_kernel(tc, hidden_states, conv_w, norm_w, out):
                 op0=ALU.add,
                 op1=ALU.add,
             )
+
+        def inverse(m):
             rinv[m] = small.tile([P, 1], F32, tag="rinv", name="rinv%d" % m)
-            nc.gpsimd.tensor_tensor(out=rinv[m][:], in0=tot[m][:], in1=neg_half[:], op=ALU.pow)
+            nc.scalar.activation(out=rinv[m][:], in_=tot[m][:], func=ACT.Abs_reciprocal_sqrt)
 
         def final(m, b):
             if b == 0:
@@ -278,12 +281,17 @@ def tile_conv2dlinalgrmsnorm_kernel(tc, hidden_states, conv_w, norm_w, out):
         for m in range(TILES + 1):
             if m < TILES:
                 sumsq(m, 0)
+            if m >= 1:
+                inverse(m - 1)
+            if m < TILES:
                 sumsq(m, 1)
-                chain(m)
             if m >= 1:
                 final(m - 1, 0)
                 if m == TILES:
                     store(m - 1, 0, 512)
+            if m < TILES:
+                total(m)
+            if m >= 1:
                 final(m - 1, 1)
                 if m == TILES:
                     store(m - 1, 512, 1024)

@@ -104,11 +104,13 @@ def tile_conv2dlinalgrmsnorm_kernel(tc, hidden_states, conv_w, norm_w, out):
 
         def w_quant(c, groups, g):
             b, jp = divmod(c, 2)
-            nc.vector.quantize_mx(
-                out=wc[(b, g)][:, 256 * jp : 256 * jp + 256].bitcast(FP8X4),
-                scales=ws[(b, g)][:, 256 * jp : 256 * jp + 256],
-                in_=groups[g][:],
-            )
+            for j in range(2):
+                lo = 256 * j + 128 * jp
+                nc.vector.quantize_mx(
+                    out=wc[(b, g)][:, lo : lo + 128].bitcast(FP8X4),
+                    scales=ws[(b, g)][:, lo : lo + 128],
+                    in_=groups[g][:, 512 * j : 512 * j + 512],
+                )
 
         xraws = []
         for a in range(4):
@@ -169,9 +171,9 @@ def tile_conv2dlinalgrmsnorm_kernel(tc, hidden_states, conv_w, norm_w, out):
                 raw = rawp.tile([P, 4096], BF16, tag="raw", name="raw%d_%d" % (c, lp))
                 nc.sync.dma_start(
                     out=raw[:].rearrange("p (l c) -> p l c", l=2),
-                    in_=conv_w[2 * lp : 2 * lp + 2, 512 * b : 512 * b + 512, :].rearrange(
-                        "l (p j) h -> p l (j h)", j=4
-                    )[:, :, 2048 * jp : 2048 * jp + 2048],
+                    in_=conv_w[2 * lp : 2 * lp + 2, 256 * c : 256 * c + 256, :].rearrange(
+                        "l (p j) h -> p l (j h)", j=2
+                    ),
                 )
                 raws.append(raw)
             banks = [psum.tile([P, 512], F32, tag="bank", name="wb%d_%d" % (c, beta)) for beta in range(4)]
@@ -261,10 +263,10 @@ def tile_conv2dlinalgrmsnorm_kernel(tc, hidden_states, conv_w, norm_w, out):
             if b == 0:
                 osb[m] = outp.tile([P, 1024], F32, tag="osb", name="osb%d" % m)
             nc.vector.scalar_tensor_tensor(
-                out=osb[m][:, 512 * b : 512 * b + 512].rearrange("t (p j) -> t p j", j=4),
-                in0=acc[(m, b)][:].rearrange("t (j p) -> t p j", j=4),
+                out=osb[m][:, 512 * b : 512 * b + 512].rearrange("t (q j) -> t q j", j=2),
+                in0=acc[(m, b)][:].rearrange("t (j q) -> t q j", j=2),
                 scalar=rinv[m][:, 0:1],
-                in1=nw[:, 512 * b : 512 * b + 512].rearrange("t (p j) -> t p j", j=4),
+                in1=nw[:, 512 * b : 512 * b + 512].rearrange("t (q j) -> t q j", j=2),
                 op0=ALU.mult,
                 op1=ALU.mult,
             )

@@ -19,9 +19,11 @@ TOKENS = 2048
 EPS = 1e-06
 FLOPS = 2 * TOKENS * H * N
 
-LEAD = 4
 TILES = 16
-PLAIN_F32 = (0, 0, 0, 0, 0)
+EARLY = 8
+PLANS = ("SPPPPD", "SPPPPD", "SPPPPD", "SPSPPDD")
+AHEAD = (1, 2, 3, 4)
+AHEAD_LAST = (5, 6)
 
 
 def perm_read(ap, c):
@@ -38,29 +40,43 @@ def tile_conv2dlinalgrmsnorm_kernel(tc, hidden_states, conv_w, norm_w, out):
     out_flat = out.flatten_outer_dims()
     with ExitStack() as ctx:
         const = ctx.enter_context(tc.tile_pool(name="const", bufs=1))
-        rawp = ctx.enter_context(tc.tile_pool(name="rawp", bufs=8))
+        rawp = ctx.enter_context(tc.tile_pool(name="rawp", bufs=10))
         bigp = ctx.enter_context(tc.tile_pool(name="bigp", bufs=6))
         outp = ctx.enter_context(tc.tile_pool(name="outp", bufs=4))
         grpp = ctx.enter_context(tc.tile_pool(name="grpp", bufs=4))
         xcp = ctx.enter_context(tc.tile_pool(name="xcp", bufs=16))
         junkp = ctx.enter_context(tc.tile_pool(name="junkp", bufs=2))
-        small = ctx.enter_context(tc.tile_pool(name="small", bufs=4))
-        psum = ctx.enter_context(tc.psum_pool(name="psum", bufs=8))
+        small = ctx.enter_context(tc.tile_pool(name="small", bufs=12))
+        psum = ctx.enter_context(tc.psum_pool(name="psum", bufs=1))
         ctx.enter_context(tc.manual_schedule())
 
+        def bank(i, name):
+            return psum.tile([P, 512], F32, tag="bank%d" % i, name=name)
+
+        xraws = {}
+
+        def load_x(a):
+            xraws[a] = rawp.tile([P, 4096], BF16, tag="raw", name="xraw%d" % a)
+            nc.sync.dma_start(
+                out=xraws[a][:],
+                in_=x_flat[512 * a : 512 * a + 512, :].rearrange("(p i) h -> p (i h)", i=4),
+            )
+
+        warm = const.tile([P, 1], F32)
+        nc.vector.memset(warm[:], 1.0)
+        nc.scalar.activation(out=warm[:], in_=warm[:], func=ACT.Abs_reciprocal_sqrt)
+        for a in range(EARLY // 4):
+            load_x(a)
         nw_row = const.tile([P, N], BF16)
         nc.vector.memset(nw_row[:], 0.0)
         nc.sync.dma_start(out=nw_row[0:1, :], in_=norm_w.rearrange("(o n) -> o n", o=1))
         ones = const.tile([P, P], BF16)
         nc.vector.memset(ones[:], 1.0)
         nw = const.tile([P, N], BF16)
-        warm = const.tile([P, 1], F32)
-        nc.vector.memset(warm[:], 1.0)
-        nc.scalar.activation(out=warm[:], in_=warm[:], func=ACT.Abs_reciprocal_sqrt)
-        ident_bf = const.tile([P, P], BF16)
-        make_identity(nc, ident_bf[:])
         ident = const.tile([P, P], F32)
         make_identity(nc, ident[:])
+        ident_bf = const.tile([P, P], BF16)
+        make_identity(nc, ident_bf[:])
 
         wc = {}
         ws = {}
@@ -69,72 +85,15 @@ def tile_conv2dlinalgrmsnorm_kernel(tc, hidden_states, conv_w, norm_w, out):
                 wc[(b, g)] = const.tile([P, 512], U32, name="wc%d%d" % (b, g), align_bytes=64)
                 ws[(b, g)] = const.tile([P, 512], U8, name="ws%d%d" % (b, g), align_bytes=64)
 
-        def w_run(c, k, src, direct, banks):
-            if k < 4:
-                for beta in range(4):
-                    g, j = divmod(beta, 2)
-                    base = j * 1024 + g * 512 + (k // 2) * 256
-                    nc.tensor.matmul(
-                        out=banks[beta][:, 128 * k : 128 * k + 128],
-                        lhsT=direct[:, base : base + 256].rearrange("p (q e) -> p e q", e=2)[:, k % 2, :],
-                        rhs=ident_bf[:],
-                        start=(k == 0),
-                        stop=False,
-                    )
-            n_plain = 0 if (c == 3 and k == 4) else PLAIN_F32[k]
-            for beta in range(4):
-                g, j = divmod(beta, 2)
-                for t in range(4):
-                    col = (j * 8 + g * 4 + t) * 128
-                    nc.tensor.matmul(
-                        out=banks[beta][:, 128 * t : 128 * t + 128],
-                        lhsT=src[:, col : col + 128],
-                        rhs=ident[:],
-                        start=False,
-                        stop=(k == 4 and t == 3),
-                        is_transpose=(4 * beta + t >= n_plain),
-                    )
-
-        def w_evac(banks, groups, beta):
-            g, j = divmod(beta, 2)
-            nc.scalar.copy(
-                out=groups[g][:, 512 * j : 512 * j + 512].rearrange("p (n t) -> p n t", t=4),
-                in_=banks[beta][:].rearrange("p (t n) -> p n t", t=4),
-            )
-
-        def w_quant(c, groups, g):
-            b, jp = divmod(c, 2)
-            for j in range(2):
-                lo = 256 * j + 128 * jp
-                nc.vector.quantize_mx(
-                    out=wc[(b, g)][:, lo : lo + 128].bitcast(FP8X4),
-                    scales=ws[(b, g)][:, lo : lo + 128],
-                    in_=groups[g][:, 512 * j : 512 * j + 512],
-                )
-
-        xraws = []
-        for a in range(4):
-            xraw = rawp.tile([P, 4096], BF16, tag="raw", name="xraw%d" % a)
-            nc.sync.dma_start(
-                out=xraw[:],
-                in_=x_flat[512 * a : 512 * a + 512, :].rearrange("(p i) h -> p (i h)", i=4),
-            )
-            xraws.append(xraw)
-
         xt = {}
         xg = {}
         xc = {}
         xs = {}
-        acc = {}
-        ss = {}
-        tot = {}
-        rinv = {}
-        osb = {}
 
-        def x_t(m):
+        def x_t(m, i_bank):
             a, i = divmod(m, 4)
             xw = xraws[a][:].bitcast(F32)
-            xt[m] = psum.tile([P, 512], F32, tag="bank", name="xt%d" % m)
+            xt[m] = bank(i_bank, "xt%d" % m)
             for cc in range(4):
                 nc.tensor.transpose(
                     xt[m][:, 128 * cc : 128 * cc + 128],
@@ -142,11 +101,11 @@ def tile_conv2dlinalgrmsnorm_kernel(tc, hidden_states, conv_w, norm_w, out):
                     ident[:],
                 )
 
-        def x_evac(m):
+        def x_evac(m, on_vector):
             xg[m] = grpp.tile([P, 1024], BF16, tag="xgrp", name="xg%d" % m, align_bytes=64)
             dst = xg[m][:].bitcast(F32).rearrange("p (g r u) -> p g r u", g=2, u=2)
             src = xt[m][:].rearrange("p (g u r) -> p g r u", g=2, u=2)
-            if m % 3 == 2:
+            if on_vector:
                 nc.vector.tensor_copy(out=dst, in_=src)
             else:
                 nc.scalar.copy(out=dst, in_=src)
@@ -156,85 +115,33 @@ def tile_conv2dlinalgrmsnorm_kernel(tc, hidden_states, conv_w, norm_w, out):
             xs[m] = xcp.tile([P, 256], U8, tag="xs", name="xs%d" % m, align_bytes=64)
             nc.vector.quantize_mx(out=xc[m][:].bitcast(FP8X4), scales=xs[m][:], in_=xg[m][:])
 
-        for k in range(TILES):
-            x_t(k)
-            x_evac(k)
-            if k >= 1:
-                x_quant(k - 1)
-        x_quant(TILES - 1)
+        acc = {}
+        ss = {}
+        tot = {}
+        rinv = {}
+        osb = {}
 
-        prev = None
-        for c in range(4):
-            b, jp = divmod(c, 2)
-            raws = []
-            for lp in range(5):
-                raw = rawp.tile([P, 4096], BF16, tag="raw", name="raw%d_%d" % (c, lp))
-                nc.sync.dma_start(
-                    out=raw[:].rearrange("p (l c) -> p l c", l=2),
-                    in_=conv_w[2 * lp : 2 * lp + 2, 256 * c : 256 * c + 256, :].rearrange(
-                        "l (p j) h -> p l (j h)", j=2
-                    ),
-                )
-                raws.append(raw)
-            banks = [psum.tile([P, 512], F32, tag="bank", name="wb%d_%d" % (c, beta)) for beta in range(4)]
-            groups = [
-                grpp.tile([P, 1024], BF16, tag="wgrp", name="wg%d_%d" % (c, g), align_bytes=64) for g in range(2)
-            ]
-            single = bigp.tile([P, 2048], F32, tag="big", name="single%d" % c)
-            nc.scalar.copy(out=split_write(single[:], 8), in_=perm_read(raws[0][:, 2048:4096], 8))
-            if prev is not None:
-                for beta in range(4):
-                    w_evac(prev[0], prev[1], beta)
-            w_run(c, 0, single, raws[0], banks)
-            if c == 0:
-                for b2 in range(2):
-                    spread = psum.tile([P, 512], F32, tag="bank", name="spread%d" % b2)
-                    nc.tensor.matmul(
-                        out=spread[:], lhsT=ones[:], rhs=nw_row[:, 512 * b2 : 512 * b2 + 512], start=True, stop=True
-                    )
-                    nc.scalar.copy(out=nw[:, 512 * b2 : 512 * b2 + 512], in_=spread[:])
-            for lp in range(1, 5):
-                pair = bigp.tile([P, 2048], F32, tag="big", name="pair%d_%d" % (c, lp))
-                if c == 3 and lp == 4:
-                    for beta in range(4):
-                        g, j = divmod(beta, 2)
-                        lo = j * 1024 + g * 512
-                        nc.vector.tensor_tensor(
-                            out=split_write(pair[:, lo : lo + 512], 2),
-                            in0=perm_read(raws[lp][:, lo : lo + 512], 2),
-                            in1=perm_read(raws[lp][:, 2048 + lo : 2048 + lo + 512], 2),
-                            op=ALU.add,
-                        )
-                else:
-                    nc.vector.tensor_tensor(
-                        out=split_write(pair[:], 8),
-                        in0=perm_read(raws[lp][:, 0:2048], 8),
-                        in1=perm_read(raws[lp][:, 2048:4096], 8),
-                        op=ALU.add,
-                    )
-                if lp == 1 and prev is not None:
-                    w_quant(c - 1, prev[1], 0)
-                    w_quant(c - 1, prev[1], 1)
-                w_run(c, lp, pair, raws[0], banks)
-            prev = (banks, groups)
-        for beta in range(4):
-            w_evac(prev[0], prev[1], beta)
-            if beta % 2 == 1:
-                w_quant(3, prev[1], beta // 2)
+        where = {}
 
-        def mx(m):
-            for b in range(2):
-                acc[(m, b)] = psum.tile([P, 512], F32, tag="bank", name="acc%d_%d" % (m, b))
-                for g in range(2):
-                    nc.tensor.matmul_mx(
-                        out=acc[(m, b)][:],
-                        lhsT=xc[m][:, 128 * g : 128 * g + 128].bitcast(FP8X4),
-                        lhsT_scale=xs[m][:, 128 * g : 128 * g + 128],
-                        rhs=wc[(b, g)][:].bitcast(FP8X4),
-                        rhs_scale=ws[(b, g)][:],
-                        start=(g == 0),
-                        stop=(g == 1),
-                    )
+        def mx_open(m, b, i_bank):
+            where[(m, b)] = i_bank
+            acc[(m, b)] = bank(i_bank, "acc%d_%d" % (m, b))
+
+        def mx_pass(m, b, g):
+            nc.tensor.matmul_mx(
+                out=acc[(m, b)][:],
+                lhsT=xc[m][:, 128 * g : 128 * g + 128].bitcast(FP8X4),
+                lhsT_scale=xs[m][:, 128 * g : 128 * g + 128],
+                rhs=wc[(b, g)][:].bitcast(FP8X4),
+                rhs_scale=ws[(b, g)][:],
+                start=(g == 0),
+                stop=(g == 1),
+            )
+
+        def mx(m, b, i_bank):
+            mx_open(m, b, i_bank)
+            for g in range(2):
+                mx_pass(m, b, g)
 
         def sumsq(m, b):
             if b == 0:
@@ -242,6 +149,17 @@ def tile_conv2dlinalgrmsnorm_kernel(tc, hidden_states, conv_w, norm_w, out):
             junk = junkp.tile([P, 512], BF16, tag="junk", name="junk%d_%d" % (m, b))
             nc.scalar.activation(
                 out=junk[:], in_=acc[(m, b)][:], func=ACT.Square, scale=1.0 / 32.0, accum_out=ss[m][:, b : b + 1]
+            )
+
+        z0 = {}
+
+        def ahead_scale(m):
+            z0[m] = const.tile([P, 512], F32, name="z0_%d" % m)
+            nc.vector.tensor_tensor(
+                out=z0[m][:].rearrange("t (q j) -> t q j", j=2),
+                in0=acc[(m, 0)][:].rearrange("t (j q) -> t q j", j=2),
+                in1=nw[:, 0:512].rearrange("t (q j) -> t q j", j=2),
+                op=ALU.mult,
             )
 
         def total(m):
@@ -262,6 +180,16 @@ def tile_conv2dlinalgrmsnorm_kernel(tc, hidden_states, conv_w, norm_w, out):
         def final(m, b):
             if b == 0:
                 osb[m] = outp.tile([P, 1024], F32, tag="osb", name="osb%d" % m)
+            if b == 0 and m in z0:
+                nc.gpsimd.tensor_scalar(
+                    out=osb[m][:, 0:512],
+                    in0=z0[m][:],
+                    scalar1=rinv[m][:, 0:1],
+                    scalar2=0.0,
+                    op0=ALU.mult,
+                    op1=ALU.add,
+                )
+                return
             nc.vector.scalar_tensor_tensor(
                 out=osb[m][:, 512 * b : 512 * b + 512].rearrange("t (q j) -> t q j", j=2),
                 in0=acc[(m, b)][:].rearrange("t (j q) -> t q j", j=2),
@@ -278,26 +206,193 @@ def tile_conv2dlinalgrmsnorm_kernel(tc, hidden_states, conv_w, norm_w, out):
                 in_=osb[m][:, lo:hi],
             )
 
-        for m in range(LEAD):
-            mx(m)
+        def w_direct(raw, banks, beta, t, start, stop):
+            g, j = divmod(beta, 2)
+            base = j * 1024 + g * 512 + (t // 2) * 256
+            nc.tensor.matmul(
+                out=banks[beta][:, 128 * t : 128 * t + 128],
+                lhsT=raw[:, base : base + 256].rearrange("p (q e) -> p e q", e=2)[:, t % 2, :],
+                rhs=ident_bf[:],
+                start=start,
+                stop=stop,
+            )
+
+        def w_turn(src, banks, beta, first, last):
+            g, j = divmod(beta, 2)
+            for t in range(4):
+                col = (j * 8 + g * 4 + t) * 128
+                nc.tensor.matmul(
+                    out=banks[beta][:, 128 * t : 128 * t + 128],
+                    lhsT=src[:, col : col + 128],
+                    rhs=ident[:],
+                    start=(first and t == 0),
+                    stop=(last and t == 3),
+                    is_transpose=True,
+                )
+
+        def w_evac(chunk, beta, on_vector):
+            g, j = divmod(beta, 2)
+            dst = chunk["groups"][g][:, 512 * j : 512 * j + 512].rearrange("p (n t) -> p n t", t=4)
+            src = chunk["banks"][beta][:].rearrange("p (t n) -> p n t", t=4)
+            if on_vector:
+                nc.vector.tensor_copy(out=dst, in_=src)
+            else:
+                nc.scalar.copy(out=dst, in_=src)
+
+        def w_quant(chunk, beta):
+            g, j = divmod(beta, 2)
+            b, jp = divmod(chunk["c"], 2)
+            lo = 256 * j + 128 * jp
+            nc.vector.quantize_mx(
+                out=wc[(b, g)][:, lo : lo + 128].bitcast(FP8X4),
+                scales=ws[(b, g)][:, lo : lo + 128],
+                in_=chunk["groups"][g][:, 512 * j : 512 * j + 512],
+            )
+
+        def w_load(c, l0, n_l):
+            raw = rawp.tile([P, 2048 * n_l], BF16, tag="raw", name="raw%d_%d" % (c, l0))
+            nc.sync.dma_start(
+                out=raw[:].rearrange("p (l c) -> p l c", l=n_l),
+                in_=conv_w[l0 : l0 + n_l, 256 * c : 256 * c + 256, :].rearrange("l (p j) h -> p l (j h)", j=2),
+            )
+            return raw
+
+        def w_add(dst, raw, parts):
+            width = 2048 // parts
+            for lo in range(0, 2048, width):
+                nc.vector.tensor_tensor(
+                    out=split_write(dst[:, lo : lo + width], width // 256),
+                    in0=perm_read(raw[:, lo : lo + width], width // 256),
+                    in1=perm_read(raw[:, 2048 + lo : 2048 + lo + width], width // 256),
+                    op=ALU.add,
+                )
+
+        for k in range(EARLY):
+            x_t(k, k % 8)
+            x_evac(k, k % 3 == 2)
+            if k >= 1:
+                x_quant(k - 1)
+        x_quant(EARLY - 1)
+        for b2 in range(2):
+            spread = bank(4 + b2, "spread%d" % b2)
+            nc.tensor.matmul(
+                out=spread[:], lhsT=ones[:], rhs=nw_row[:, 512 * b2 : 512 * b2 + 512], start=True, stop=True
+            )
+            nc.scalar.copy(out=nw[:, 512 * b2 : 512 * b2 + 512], in_=spread[:])
+
+        prev = None
+        for c in range(4):
+            plan = PLANS[c]
+            chunk = {
+                "c": c,
+                "banks": [bank(4 * (c % 2) + beta, "wb%d_%d" % (c, beta)) for beta in range(4)],
+                "groups": [
+                    grpp.tile([P, 1024], BF16, tag="wgrp", name="wg%d_%d" % (c, g), align_bytes=64) for g in range(2)
+                ],
+            }
+            layer = 0
+            pairs = 0
+            for k, kind in enumerate(plan):
+                first = k == 0
+                last = k == len(plan) - 1
+                raw = w_load(c, layer, 2 if kind == "P" else 1)
+                if kind == "D":
+                    for beta in range(4):
+                        for t in range(4):
+                            w_direct(raw, chunk["banks"], beta, t, False, last and t == 3)
+                else:
+                    src = bigp.tile([P, 2048], F32, tag="big", name="src%d_%d" % (c, k))
+                    if kind == "S":
+                        nc.scalar.copy(out=split_write(src[:], 8), in_=perm_read(raw[:], 8))
+                    else:
+                        pairs += 1
+                        w_add(src, raw, 4 if c == 3 and pairs == 3 else 1)
+                    for beta in range(4):
+                        w_turn(src, chunk["banks"], beta, first, False)
+                if kind == "S" and first and prev is not None:
+                    for beta in range(4):
+                        w_evac(prev, beta, False)
+                if kind == "P" and pairs == 1 and prev is not None:
+                    for beta in range(4):
+                        w_quant(prev, beta)
+                if c == 2 and k == 1:
+                    for i, m in enumerate(AHEAD):
+                        mx(m, 0, 4 + i)
+                    for m in AHEAD:
+                        sumsq(m, 0)
+                if c == 2 and k == 4:
+                    for m in AHEAD:
+                        ahead_scale(m)
+                if c == 3 and k == 0:
+                    mx(0, 0, 0)
+                if c == 3 and 1 <= k <= 2:
+                    mx(AHEAD_LAST[k - 1], 0, k)
+                if c == 3 and k == 2:
+                    sumsq(0, 0)
+                    for m in AHEAD_LAST:
+                        sumsq(m, 0)
+                if c == 3 and k == 4:
+                    for m in AHEAD_LAST:
+                        ahead_scale(m)
+                layer += 2 if kind == "P" else 1
+            prev = chunk
+        for a in range(EARLY // 4, TILES // 4):
+            load_x(a)
+        w_evac(chunk, 0, False)
+        w_evac(chunk, 1, True)
+        w_quant(chunk, 0)
+        w_evac(chunk, 2, False)
+        w_quant(chunk, 1)
+        w_evac(chunk, 3, False)
+        w_quant(chunk, 2)
+        w_quant(chunk, 3)
+
+        pending = [(m, b) for m in range(TILES) for b in range(2) if (m, b) not in acc]
+        free = list(range(1, 6))
+        begun = []
+        while free:
+            m, b = pending.pop(0)
+            mx_open(m, b, free.pop(0))
+            begun.append((m, b))
+        for few in (begun[:2], begun[2:]):
+            for g in range(2):
+                for m, b in few:
+                    mx_pass(m, b, g)
+            x_t(EARLY + (len(few) > 2), 6 + (len(few) > 2))
         for m in range(TILES + 1):
-            if m < TILES:
+            both = m < TILES and m not in z0 and m >= 1
+            if both:
                 sumsq(m, 0)
-            if m >= 1:
-                inverse(m - 1)
+                if m >= 2:
+                    inverse(m - 1)
             if m < TILES:
                 sumsq(m, 1)
+            if m >= 2 and not both:
+                inverse(m - 1)
+            if m == 0:
+                total(0)
+                inverse(0)
             if m >= 1:
                 final(m - 1, 0)
-                if m == TILES:
+                if m == TILES or m == 1:
                     store(m - 1, 0, 512)
-            if m < TILES:
+            if 1 <= m < TILES:
                 total(m)
             if m >= 1:
                 final(m - 1, 1)
-                if m == TILES:
+                if m == TILES or m == 1:
                     store(m - 1, 512, 1024)
                 else:
                     store(m - 1, 0, 1024)
-            if m >= 1 and m - 1 + LEAD < TILES:
-                mx(m - 1 + LEAD)
+                if m - 1 not in z0:
+                    free.append(where[(m - 1, 0)])
+                free.append(where[(m - 1, 1)])
+            if m >= 2 and EARLY + m - 2 < TILES:
+                x_quant(EARLY + m - 2)
+            if m >= 1 and EARLY + m - 1 < TILES:
+                x_evac(EARLY + m - 1, m % 4 == 3)
+                if EARLY + m + 1 < TILES:
+                    x_t(EARLY + m + 1, 6 + (m - 1) % 2)
+            while free and pending and pending[0][0] in xc:
+                mx(pending[0][0], pending[0][1], free.pop(0))
+                pending.pop(0)

@@ -69,7 +69,7 @@ def tile_conv2dlinalgrmsnorm_kernel(tc, hidden_states, conv_w, norm_w, out):
             load_x(a)
         nw_row = const.tile([P, N], BF16)
         nc.vector.memset(nw_row[:], 0.0)
-        nc.sync.dma_start(out=nw_row[0:1, :], in_=norm_w.rearrange("(o n) -> o n", o=1))
+        nc.scalar.dma_start(out=nw_row[0:1, :], in_=norm_w.rearrange("(o n) -> o n", o=1))
         ones = const.tile([P, P], BF16)
         nc.vector.memset(ones[:], 1.0)
         nw = const.tile([P, N], BF16)
@@ -181,13 +181,12 @@ def tile_conv2dlinalgrmsnorm_kernel(tc, hidden_states, conv_w, norm_w, out):
             if b == 0:
                 osb[m] = outp.tile([P, 1024], F32, tag="osb", name="osb%d" % m)
             if b == 0 and m in z0:
-                nc.gpsimd.tensor_scalar(
+                nc.vector.tensor_scalar(
                     out=osb[m][:, 0:512],
                     in0=z0[m][:],
                     scalar1=rinv[m][:, 0:1],
-                    scalar2=0.0,
+                    scalar2=None,
                     op0=ALU.mult,
-                    op1=ALU.add,
                 )
                 return
             nc.vector.scalar_tensor_tensor(
@@ -273,13 +272,6 @@ def tile_conv2dlinalgrmsnorm_kernel(tc, hidden_states, conv_w, norm_w, out):
             if k >= 1:
                 x_quant(k - 1)
         x_quant(EARLY - 1)
-        for b2 in range(2):
-            spread = bank(4 + b2, "spread%d" % b2)
-            nc.tensor.matmul(
-                out=spread[:], lhsT=ones[:], rhs=nw_row[:, 512 * b2 : 512 * b2 + 512], start=True, stop=True
-            )
-            nc.scalar.copy(out=nw[:, 512 * b2 : 512 * b2 + 512], in_=spread[:])
-
         prev = None
         for c in range(4):
             plan = PLANS[c]
@@ -315,6 +307,13 @@ def tile_conv2dlinalgrmsnorm_kernel(tc, hidden_states, conv_w, norm_w, out):
                 if kind == "P" and pairs == 1 and prev is not None:
                     for beta in range(4):
                         w_quant(prev, beta)
+                if c == 0 and k == 1:
+                    for b2 in range(2):
+                        spread = bank(4 + b2, "spread%d" % b2)
+                        nc.tensor.matmul(
+                            out=spread[:], lhsT=ones[:], rhs=nw_row[:, 512 * b2 : 512 * b2 + 512], start=True, stop=True
+                        )
+                        nc.scalar.copy(out=nw[:, 512 * b2 : 512 * b2 + 512], in_=spread[:])
                 if c == 2 and k == 1:
                     for i, m in enumerate(AHEAD):
                         mx(m, 0, 4 + i)

@@ -21,9 +21,10 @@ FLOPS = 2 * TOKENS * H * N
 
 TILES = 16
 EARLY = 8
-PLANS = ("SPPPPD", "SPPPPD", "SPPPPD", "SPSPPDD")
-AHEAD = (1, 2, 3, 4)
-AHEAD_LAST = (5, 6)
+LAGGED = (0, 1, 2, 3)
+PAIR_MX = {1: (), 2: (0,), 3: (1, 2), 4: (3,)}
+PAIR_SCALE = {1: (), 2: (0,), 3: (1, 2), 4: (3,)}
+PLANS = ("PxPxQPP", "QPPPP", "QPPPP", "QPPPDD")
 
 
 def perm_read(ap, c):
@@ -50,8 +51,8 @@ def tile_conv2dlinalgrmsnorm_kernel(tc, hidden_states, conv_w, norm_w, out):
         psum = ctx.enter_context(tc.psum_pool(name="psum", bufs=1))
         ctx.enter_context(tc.manual_schedule())
 
-        def bank(i, name):
-            return psum.tile([P, 512], F32, tag="bank%d" % i, name=name)
+        def bank(i, name, dtype=F32):
+            return psum.tile([P, 512 if dtype == F32 else 1024], dtype, tag="bank%d" % i, name=name)
 
         xraws = {}
 
@@ -65,18 +66,24 @@ def tile_conv2dlinalgrmsnorm_kernel(tc, hidden_states, conv_w, norm_w, out):
         warm = const.tile([P, 1], F32)
         nc.vector.memset(warm[:], 1.0)
         nc.scalar.activation(out=warm[:], in_=warm[:], func=ACT.Abs_reciprocal_sqrt)
-        for a in range(EARLY // 4):
-            load_x(a)
-        nw_row = const.tile([P, N], BF16)
-        nc.vector.memset(nw_row[:], 0.0)
-        nc.scalar.dma_start(out=nw_row[0:1, :], in_=norm_w.rearrange("(o n) -> o n", o=1))
-        ones = const.tile([P, P], BF16)
-        nc.vector.memset(ones[:], 1.0)
+        nw_rows = const.tile([P, P], BF16)
+        nc.vector.memset(nw_rows[:], 0.0)
+        nc.scalar.dma_start(out=nw_rows[0:8, :], in_=norm_w.rearrange("(m j) -> m j", m=8))
         nw = const.tile([P, N], BF16)
         ident = const.tile([P, P], F32)
         make_identity(nc, ident[:])
         ident_bf = const.tile([P, P], BF16)
         make_identity(nc, ident_bf[:])
+        turn_f = const.tile([P, P], F32)
+        nc.vector.tensor_copy(
+            out=turn_f[:].rearrange("p (s q) -> p s q", s=2), in_=ident[:].rearrange("p (q s) -> p s q", s=2)
+        )
+        turn_b = const.tile([P, P], BF16)
+        nc.vector.tensor_copy(
+            out=turn_b[:].rearrange("p (s q) -> p s q", s=2), in_=ident_bf[:].rearrange("p (q s) -> p s q", s=2)
+        )
+        both_b = const.tile([P, 64], BF16)
+        nc.vector.tensor_tensor(out=both_b[:], in0=ident_bf[:, 0:64], in1=ident_bf[:, 64:128], op=ALU.add)
 
         wc = {}
         ws = {}
@@ -143,23 +150,58 @@ def tile_conv2dlinalgrmsnorm_kernel(tc, hidden_states, conv_w, norm_w, out):
             for g in range(2):
                 mx_pass(m, b, g)
 
-        def sumsq(m, b):
-            if b == 0:
-                ss[m] = small.tile([P, 2], F32, tag="ss", name="ss%d" % m)
-            junk = junkp.tile([P, 512], BF16, tag="junk", name="junk%d_%d" % (m, b))
+        def square(src, accum, name):
+            junk = junkp.tile([P, 512], BF16, tag="junk", name=name)
+            width = src.shape[1]
             nc.scalar.activation(
-                out=junk[:], in_=acc[(m, b)][:], func=ACT.Square, scale=1.0 / 32.0, accum_out=ss[m][:, b : b + 1]
+                out=junk[:, 0:width], in_=src, func=ACT.Square, scale=1.0 / 32.0, accum_out=accum
             )
 
-        z0 = {}
+        def sumsq(m, b):
+            if m not in ss:
+                ss[m] = small.tile([P, 2], F32, tag="ss", name="ss%d" % m)
+            square(acc[(m, b)][:], ss[m][:, b : b + 1], "junk%d_%d" % (m, b))
 
-        def ahead_scale(m):
+        early_ss = [const.tile([P, EARLY], F32, name="early_ss%d" % h) for h in range(2)]
+        early_tot = const.tile([P, EARLY], F32)
+        z0 = {}
+        for m in range(EARLY):
             z0[m] = const.tile([P, 512], F32, name="z0_%d" % m)
-            nc.vector.tensor_tensor(
-                out=z0[m][:].rearrange("t (q j) -> t q j", j=2),
-                in0=acc[(m, 0)][:].rearrange("t (j q) -> t q j", j=2),
-                in1=nw[:, 0:512].rearrange("t (q j) -> t q j", j=2),
-                op=ALU.mult,
+        ahead = {}
+
+        def ahead_mx(m, h, i_bank):
+            if m % 2 == 0:
+                ahead[i_bank] = bank(i_bank, "ahead%d_%d" % (h, m))
+            for g in range(2):
+                nc.tensor.matmul_mx(
+                    out=ahead[i_bank][:, 256 * (m % 2) : 256 * (m % 2) + 256],
+                    lhsT=xc[m][:, 128 * g : 128 * g + 128].bitcast(FP8X4),
+                    lhsT_scale=xs[m][:, 128 * g : 128 * g + 128],
+                    rhs=wc[(0, g)][:, 256 * h : 256 * h + 256].bitcast(FP8X4),
+                    rhs_scale=ws[(0, g)][:, 256 * h : 256 * h + 256],
+                    start=(g == 0),
+                    stop=(g == 1),
+                )
+
+        def ahead_square(m, h, i_bank):
+            lo = 256 * (m % 2)
+            square(ahead[i_bank][:, lo : lo + 256], early_ss[h][:, m : m + 1], "ajunk%d_%d" % (h, m))
+
+        def ahead_scale(m, h, i_bank):
+            lo = 256 * (m % 2)
+            nc.scalar.copy(
+                out=z0[m][:, 256 * h : 256 * h + 256].rearrange("t (q j) -> t q j", j=2),
+                in_=ahead[i_bank][:, lo : lo + 256].rearrange("t (j q) -> t q j", j=2),
+            )
+
+        def early_total():
+            nc.vector.scalar_tensor_tensor(
+                out=early_tot[:],
+                in0=early_ss[0][:],
+                scalar=EPS * L * L,
+                in1=early_ss[1][:],
+                op0=ALU.add,
+                op1=ALU.add,
             )
 
         def total(m):
@@ -175,28 +217,46 @@ def tile_conv2dlinalgrmsnorm_kernel(tc, hidden_states, conv_w, norm_w, out):
 
         def inverse(m):
             rinv[m] = small.tile([P, 1], F32, tag="rinv", name="rinv%d" % m)
-            nc.scalar.activation(out=rinv[m][:], in_=tot[m][:], func=ACT.Abs_reciprocal_sqrt)
+            if m < EARLY:
+                nc.scalar.activation(
+                    out=rinv[m][:], in_=ss[m][:, 1:2], func=ACT.Abs_reciprocal_sqrt, bias=early_tot[:, m : m + 1]
+                )
+            else:
+                nc.scalar.activation(out=rinv[m][:], in_=tot[m][:], func=ACT.Abs_reciprocal_sqrt)
 
         def final(m, b):
             if b == 0:
                 osb[m] = outp.tile([P, 1024], F32, tag="osb", name="osb%d" % m)
-            if b == 0 and m in z0:
-                nc.vector.tensor_scalar(
-                    out=osb[m][:, 0:512],
-                    in0=z0[m][:],
-                    scalar1=rinv[m][:, 0:1],
-                    scalar2=None,
+                if m < EARLY:
+                    if m in LAGGED:
+                        nc.vector.tensor_scalar(
+                            out=osb[m][:, 0:512],
+                            in0=z0[m][:],
+                            scalar1=rinv[m][:, 0:1],
+                            scalar2=None,
+                            op0=ALU.mult,
+                        )
+                    else:
+                        nc.vector.scalar_tensor_tensor(
+                            out=osb[m][:, 0:512],
+                            in0=z0[m][:],
+                            scalar=rinv[m][:, 0:1],
+                            in1=nw[:, 0:512],
+                            op0=ALU.mult,
+                            op1=ALU.mult,
+                        )
+                    return
+            width = 256 if b == 0 else 512
+            for lo in range(0, 512, width):
+                at = 512 * b + lo
+                nc.vector.scalar_tensor_tensor(
+                    out=osb[m][:, at : at + width].rearrange("t (q j) -> t q j", j=2),
+                    in0=acc[(m, b)][:, lo : lo + width].rearrange("t (j q) -> t q j", j=2),
+                    scalar=rinv[m][:, 0:1],
+                    in1=nw[:, at : at + width].rearrange("t (q j) -> t q j", j=2),
                     op0=ALU.mult,
+                    op1=ALU.mult,
                 )
-                return
-            nc.vector.scalar_tensor_tensor(
-                out=osb[m][:, 512 * b : 512 * b + 512].rearrange("t (q j) -> t q j", j=2),
-                in0=acc[(m, b)][:].rearrange("t (j q) -> t q j", j=2),
-                scalar=rinv[m][:, 0:1],
-                in1=nw[:, 512 * b : 512 * b + 512].rearrange("t (q j) -> t q j", j=2),
-                op0=ALU.mult,
-                op1=ALU.mult,
-            )
 
         def store(m, lo, hi):
             a, i = divmod(m, 4)
@@ -205,16 +265,33 @@ def tile_conv2dlinalgrmsnorm_kernel(tc, hidden_states, conv_w, norm_w, out):
                 in_=osb[m][:, lo:hi],
             )
 
-        def w_direct(raw, banks, beta, t, start, stop):
+        def block(raw, row, g, t):
+            base = row * 1024 + g * 512 + (t // 2) * 256
+            return raw[:, base : base + 256].rearrange("p (q e) -> p e q", e=2)[:, t % 2, :]
+
+        def w_direct(raw, banks, beta, stop):
             g, j = divmod(beta, 2)
-            base = j * 1024 + g * 512 + (t // 2) * 256
-            nc.tensor.matmul(
-                out=banks[beta][:, 128 * t : 128 * t + 128],
-                lhsT=raw[:, base : base + 256].rearrange("p (q e) -> p e q", e=2)[:, t % 2, :],
-                rhs=ident_bf[:],
-                start=start,
-                stop=stop,
-            )
+            for t in range(4):
+                nc.tensor.matmul(
+                    out=banks[beta][:, 128 * t : 128 * t + 128],
+                    lhsT=block(raw, j, g, t),
+                    rhs=turn_b[:],
+                    start=False,
+                    stop=(stop and t == 3),
+                )
+
+        def w_two(raw, banks, beta, first):
+            g, j = divmod(beta, 2)
+            for t in range(4):
+                for s in range(2):
+                    lo = 128 * t + 64 * s
+                    nc.tensor.matmul(
+                        out=banks[beta][:, lo : lo + 64],
+                        lhsT=block(raw, 2 * s + j, g, t),
+                        rhs=both_b[:],
+                        start=(first and t == 0 and s == 0),
+                        stop=False,
+                    )
 
         def w_turn(src, banks, beta, first, last):
             g, j = divmod(beta, 2)
@@ -223,7 +300,7 @@ def tile_conv2dlinalgrmsnorm_kernel(tc, hidden_states, conv_w, norm_w, out):
                 nc.tensor.matmul(
                     out=banks[beta][:, 128 * t : 128 * t + 128],
                     lhsT=src[:, col : col + 128],
-                    rhs=ident[:],
+                    rhs=turn_f[:],
                     start=(first and t == 0),
                     stop=(last and t == 3),
                     is_transpose=True,
@@ -231,8 +308,8 @@ def tile_conv2dlinalgrmsnorm_kernel(tc, hidden_states, conv_w, norm_w, out):
 
         def w_evac(chunk, beta, on_vector):
             g, j = divmod(beta, 2)
-            dst = chunk["groups"][g][:, 512 * j : 512 * j + 512].rearrange("p (n t) -> p n t", t=4)
-            src = chunk["banks"][beta][:].rearrange("p (t n) -> p n t", t=4)
+            dst = chunk["groups"][g][:, 512 * j : 512 * j + 512].rearrange("p (q s t) -> p q s t", s=2, t=4)
+            src = chunk["banks"][beta][:].rearrange("p (t s q) -> p q s t", t=4, s=2)
             if on_vector:
                 nc.vector.tensor_copy(out=dst, in_=src)
             else:
@@ -241,7 +318,7 @@ def tile_conv2dlinalgrmsnorm_kernel(tc, hidden_states, conv_w, norm_w, out):
         def w_quant(chunk, beta):
             g, j = divmod(beta, 2)
             b, jp = divmod(chunk["c"], 2)
-            lo = 256 * j + 128 * jp
+            lo = 256 * jp + 128 * j if b == 0 else 256 * j + 128 * jp
             nc.vector.quantize_mx(
                 out=wc[(b, g)][:, lo : lo + 128].bitcast(FP8X4),
                 scales=ws[(b, g)][:, lo : lo + 128],
@@ -266,12 +343,13 @@ def tile_conv2dlinalgrmsnorm_kernel(tc, hidden_states, conv_w, norm_w, out):
                     op=ALU.add,
                 )
 
-        for k in range(EARLY):
-            x_t(k, k % 8)
-            x_evac(k, k % 3 == 2)
-            if k >= 1:
-                x_quant(k - 1)
-        x_quant(EARLY - 1)
+        def prepare(a):
+            load_x(a)
+            for i in range(4):
+                m = 4 * a + i
+                x_t(m, 4 + m % 4)
+                x_evac(m, False)
+
         prev = None
         for c in range(4):
             plan = PLANS[c]
@@ -284,59 +362,87 @@ def tile_conv2dlinalgrmsnorm_kernel(tc, hidden_states, conv_w, norm_w, out):
             }
             layer = 0
             pairs = 0
+            opened = False
+            held = None
+            tokens = 0
             for k, kind in enumerate(plan):
-                first = k == 0
                 last = k == len(plan) - 1
-                raw = w_load(c, layer, 2 if kind == "P" else 1)
-                if kind == "D":
-                    for beta in range(4):
-                        for t in range(4):
-                            w_direct(raw, chunk["banks"], beta, t, False, last and t == 3)
-                else:
-                    src = bigp.tile([P, 2048], F32, tag="big", name="src%d_%d" % (c, k))
-                    if kind == "S":
-                        nc.scalar.copy(out=split_write(src[:], 8), in_=perm_read(raw[:], 8))
-                    else:
-                        pairs += 1
-                        w_add(src, raw, 4 if c == 3 and pairs == 3 else 1)
-                    for beta in range(4):
-                        w_turn(src, chunk["banks"], beta, first, False)
-                if kind == "S" and first and prev is not None:
-                    for beta in range(4):
-                        w_evac(prev, beta, False)
-                if kind == "P" and pairs == 1 and prev is not None:
-                    for beta in range(4):
-                        w_quant(prev, beta)
-                if c == 0 and k == 1:
-                    for b2 in range(2):
-                        spread = bank(4 + b2, "spread%d" % b2)
-                        nc.tensor.matmul(
-                            out=spread[:], lhsT=ones[:], rhs=nw_row[:, 512 * b2 : 512 * b2 + 512], start=True, stop=True
+                if kind == "x":
+                    prepare(tokens)
+                    tokens += 1
+                    continue
+                if kind == "Q":
+                    raw = rawp.tile([P, 4096], BF16, tag="raw", name="raw%d_%d" % (c, layer))
+                    for half in range(2):
+                        nc.sync.dma_start(
+                            out=raw[64 * half : 64 * half + 64, :],
+                            in_=conv_w[layer + half, 256 * c : 256 * c + 256, :].rearrange("(i r) h -> i (r h)", r=4),
                         )
+                    for beta in range(4):
+                        w_two(raw, chunk["banks"], beta, not opened)
+                    opened = True
+                    layer += 2
+                    if prev is not None:
+                        for beta in range(4):
+                            w_evac(prev, beta, False)
+                elif kind == "D":
+                    raw = w_load(c, layer, 1)
+                    for beta in range(4):
+                        w_direct(raw, chunk["banks"], beta, False)
+                        if last:
+                            w_turn(held, chunk["banks"], beta, False, True)
+                    layer += 1
+                else:
+                    raw = w_load(c, layer, 2)
+                    src = bigp.tile([P, 2048], F32, tag="big", name="src%d_%d" % (c, k))
+                    pairs += 1
+                    w_add(src, raw, 4 if c == 3 and pairs == 3 else 1)
+                    if c == 3 and pairs == 3:
+                        held = src
+                    else:
+                        for beta in range(4):
+                            w_turn(src, chunk["banks"], beta, not opened, last)
+                        opened = True
+                    layer += 2
+                    if c == 0:
+                        for m in range(4 * (pairs - 2), 4 * (pairs - 1)):
+                            if 0 <= m < EARLY:
+                                x_quant(m)
+                    if pairs == 2 and prev is not None:
+                        for beta in range(4):
+                            w_quant(prev, beta)
+                if c == 0 and k == 5:
+                    nwt = bank(4, "nwt", BF16)
+                    nc.tensor.transpose(nwt[:, 0:128], nw_rows[:], ident_bf[:])
+                    nw_cols = const.tile([P, 8], F32)
+                    nc.scalar.copy(out=nw_cols[:], in_=nwt[:, 0:8])
+                    for b2 in range(2):
+                        spread = bank(5 + b2, "spread%d" % b2)
+                        for m in range(4):
+                            nc.tensor.matmul(
+                                out=spread[:, 128 * m : 128 * m + 128],
+                                lhsT=nw_cols[:, 4 * b2 + m : 4 * b2 + m + 1].to_broadcast([P, P]),
+                                rhs=ident[:],
+                                start=True,
+                                stop=True,
+                                is_transpose=True,
+                            )
                         nc.scalar.copy(out=nw[:, 512 * b2 : 512 * b2 + 512], in_=spread[:])
-                if c == 2 and k == 1:
-                    for i, m in enumerate(AHEAD):
-                        mx(m, 0, 4 + i)
-                    for m in AHEAD:
-                        sumsq(m, 0)
-                if c == 2 and k == 4:
-                    for m in AHEAD:
-                        ahead_scale(m)
-                if c == 3 and k == 0:
-                    mx(0, 0, 0)
-                if c == 3 and 1 <= k <= 2:
-                    mx(AHEAD_LAST[k - 1], 0, k)
-                if c == 3 and k == 2:
-                    sumsq(0, 0)
-                    for m in AHEAD_LAST:
-                        sumsq(m, 0)
-                if c == 3 and k == 4:
-                    for m in AHEAD_LAST:
-                        ahead_scale(m)
-                layer += 2 if kind == "P" else 1
+                if c in (1, 2) and kind == "P":
+                    for i in PAIR_MX[k]:
+                        for m in (2 * i, 2 * i + 1):
+                            ahead_mx(m, c - 1, 4 * (c - 1) + i)
+                        for m in (2 * i + 1, 2 * i):
+                            ahead_square(m, c - 1, 4 * (c - 1) + i)
+                    for i in PAIR_SCALE[k]:
+                        for m in (2 * i + 1, 2 * i):
+                            ahead_scale(m, c - 1, 4 * (c - 1) + i)
             prev = chunk
         for a in range(EARLY // 4, TILES // 4):
             load_x(a)
+        early_total()
+        for m in LAGGED[0:2]:
+            nc.vector.tensor_tensor(out=z0[m][:], in0=z0[m][:], in1=nw[:, 0:512], op=ALU.mult)
         w_evac(chunk, 0, False)
         w_evac(chunk, 1, True)
         w_quant(chunk, 0)
@@ -346,8 +452,10 @@ def tile_conv2dlinalgrmsnorm_kernel(tc, hidden_states, conv_w, norm_w, out):
         w_quant(chunk, 2)
         w_quant(chunk, 3)
 
-        pending = [(m, b) for m in range(TILES) for b in range(2) if (m, b) not in acc]
-        free = list(range(1, 6))
+        for m in LAGGED[2:4]:
+            nc.vector.tensor_tensor(out=z0[m][:], in0=z0[m][:], in1=nw[:, 0:512], op=ALU.mult)
+        pending = [(m, b) for m in range(TILES) for b in range(2) if m >= EARLY or b == 1]
+        free = list(range(0, 6))
         begun = []
         while free:
             m, b = pending.pop(0)
@@ -359,23 +467,21 @@ def tile_conv2dlinalgrmsnorm_kernel(tc, hidden_states, conv_w, norm_w, out):
                     mx_pass(m, b, g)
             x_t(EARLY + (len(few) > 2), 6 + (len(few) > 2))
         for m in range(TILES + 1):
-            both = m < TILES and m not in z0 and m >= 1
-            if both:
+            if EARLY <= m < TILES:
                 sumsq(m, 0)
-                if m >= 2:
+                if m > EARLY:
                     inverse(m - 1)
             if m < TILES:
                 sumsq(m, 1)
-            if m >= 2 and not both:
+            if m < EARLY:
+                inverse(m)
+            if m == TILES:
                 inverse(m - 1)
-            if m == 0:
-                total(0)
-                inverse(0)
             if m >= 1:
                 final(m - 1, 0)
                 if m == TILES or m == 1:
                     store(m - 1, 0, 512)
-            if 1 <= m < TILES:
+            if EARLY <= m < TILES:
                 total(m)
             if m >= 1:
                 final(m - 1, 1)
@@ -383,7 +489,7 @@ def tile_conv2dlinalgrmsnorm_kernel(tc, hidden_states, conv_w, norm_w, out):
                     store(m - 1, 512, 1024)
                 else:
                     store(m - 1, 0, 1024)
-                if m - 1 not in z0:
+                if m - 1 >= EARLY:
                     free.append(where[(m - 1, 0)])
                 free.append(where[(m - 1, 1)])
             if m >= 2 and EARLY + m - 2 < TILES:

@@ -22,9 +22,9 @@ FLOPS = 2 * TOKENS * H * N
 TILES = 16
 EARLY = 8
 LAGGED = (0, 1, 2, 3)
-PAIR_MX = {1: (), 2: (0,), 3: (1, 2), 4: (3,)}
-PAIR_SCALE = {1: (), 2: (0,), 3: (1, 2), 4: (3,)}
-PLANS = ("PxPxQPP", "QPPPP", "QPPPP", "QPPPDD")
+PAIR_MX = {1: (), 2: (0, 1), 3: (2, 3), 4: ()}
+PAIR_SCALE = {1: (), 2: (0, 1), 3: (2, 3), 4: ()}
+PLANS = ("PxPxcsDPP", "DcPPsPP", "DcPPsPP", "DcPPsPDD")
 
 
 def perm_read(ap, c):
@@ -74,17 +74,6 @@ def tile_conv2dlinalgrmsnorm_kernel(tc, hidden_states, conv_w, norm_w, out):
         make_identity(nc, ident[:])
         ident_bf = const.tile([P, P], BF16)
         make_identity(nc, ident_bf[:])
-        turn_f = const.tile([P, P], F32)
-        nc.vector.tensor_copy(
-            out=turn_f[:].rearrange("p (s q) -> p s q", s=2), in_=ident[:].rearrange("p (q s) -> p s q", s=2)
-        )
-        turn_b = const.tile([P, P], BF16)
-        nc.vector.tensor_copy(
-            out=turn_b[:].rearrange("p (s q) -> p s q", s=2), in_=ident_bf[:].rearrange("p (q s) -> p s q", s=2)
-        )
-        both_b = const.tile([P, 64], BF16)
-        nc.vector.tensor_tensor(out=both_b[:], in0=ident_bf[:, 0:64], in1=ident_bf[:, 64:128], op=ALU.add)
-
         wc = {}
         ws = {}
         for b in range(2):
@@ -269,29 +258,16 @@ def tile_conv2dlinalgrmsnorm_kernel(tc, hidden_states, conv_w, norm_w, out):
             base = row * 1024 + g * 512 + (t // 2) * 256
             return raw[:, base : base + 256].rearrange("p (q e) -> p e q", e=2)[:, t % 2, :]
 
-        def w_direct(raw, banks, beta, stop):
+        def w_direct(raw, banks, beta, first):
             g, j = divmod(beta, 2)
             for t in range(4):
                 nc.tensor.matmul(
                     out=banks[beta][:, 128 * t : 128 * t + 128],
                     lhsT=block(raw, j, g, t),
-                    rhs=turn_b[:],
-                    start=False,
-                    stop=(stop and t == 3),
+                    rhs=ident_bf[:],
+                    start=(first and t == 0),
+                    stop=False,
                 )
-
-        def w_two(raw, banks, beta, first):
-            g, j = divmod(beta, 2)
-            for t in range(4):
-                for s in range(2):
-                    lo = 128 * t + 64 * s
-                    nc.tensor.matmul(
-                        out=banks[beta][:, lo : lo + 64],
-                        lhsT=block(raw, 2 * s + j, g, t),
-                        rhs=both_b[:],
-                        start=(first and t == 0 and s == 0),
-                        stop=False,
-                    )
 
         def w_turn(src, banks, beta, first, last):
             g, j = divmod(beta, 2)
@@ -300,7 +276,7 @@ def tile_conv2dlinalgrmsnorm_kernel(tc, hidden_states, conv_w, norm_w, out):
                 nc.tensor.matmul(
                     out=banks[beta][:, 128 * t : 128 * t + 128],
                     lhsT=src[:, col : col + 128],
-                    rhs=turn_f[:],
+                    rhs=ident[:],
                     start=(first and t == 0),
                     stop=(last and t == 3),
                     is_transpose=True,
@@ -308,8 +284,8 @@ def tile_conv2dlinalgrmsnorm_kernel(tc, hidden_states, conv_w, norm_w, out):
 
         def w_evac(chunk, beta, on_vector):
             g, j = divmod(beta, 2)
-            dst = chunk["groups"][g][:, 512 * j : 512 * j + 512].rearrange("p (q s t) -> p q s t", s=2, t=4)
-            src = chunk["banks"][beta][:].rearrange("p (t s q) -> p q s t", t=4, s=2)
+            dst = chunk["groups"][g][:, 512 * j : 512 * j + 512].rearrange("p (n t) -> p n t", t=4)
+            src = chunk["banks"][beta][:].rearrange("p (t n) -> p n t", t=4)
             if on_vector:
                 nc.vector.tensor_copy(out=dst, in_=src)
             else:
@@ -371,26 +347,25 @@ def tile_conv2dlinalgrmsnorm_kernel(tc, hidden_states, conv_w, norm_w, out):
                     prepare(tokens)
                     tokens += 1
                     continue
-                if kind == "Q":
-                    raw = rawp.tile([P, 4096], BF16, tag="raw", name="raw%d_%d" % (c, layer))
-                    for half in range(2):
-                        nc.sync.dma_start(
-                            out=raw[64 * half : 64 * half + 64, :],
-                            in_=conv_w[layer + half, 256 * c : 256 * c + 256, :].rearrange("(i r) h -> i (r h)", r=4),
-                        )
+                if k == 1 and prev is not None:
                     for beta in range(4):
-                        w_two(raw, chunk["banks"], beta, not opened)
+                        w_evac(prev, beta, False)
+                if kind == "c":
+                    raw = w_load(c, layer, 1)
+                    lone = bigp.tile([P, 2048], F32, tag="big", name="src%d_%d" % (c, k))
+                    nc.scalar.copy(out=split_write(lone[:], 8), in_=perm_read(raw[:], 8))
+                    layer += 1
+                elif kind == "s":
+                    for beta in range(4):
+                        w_turn(lone, chunk["banks"], beta, not opened, False)
                     opened = True
-                    layer += 2
-                    if prev is not None:
-                        for beta in range(4):
-                            w_evac(prev, beta, False)
                 elif kind == "D":
                     raw = w_load(c, layer, 1)
                     for beta in range(4):
-                        w_direct(raw, chunk["banks"], beta, False)
+                        w_direct(raw, chunk["banks"], beta, not opened)
                         if last:
                             w_turn(held, chunk["banks"], beta, False, True)
+                    opened = True
                     layer += 1
                 else:
                     raw = w_load(c, layer, 2)
@@ -411,7 +386,7 @@ def tile_conv2dlinalgrmsnorm_kernel(tc, hidden_states, conv_w, norm_w, out):
                     if pairs == 2 and prev is not None:
                         for beta in range(4):
                             w_quant(prev, beta)
-                if c == 0 and k == 5:
+                if c == 0 and k == 7:
                     nwt = bank(4, "nwt", BF16)
                     nc.tensor.transpose(nwt[:, 0:128], nw_rows[:], ident_bf[:])
                     nw_cols = const.tile([P, 8], F32)
@@ -429,12 +404,12 @@ def tile_conv2dlinalgrmsnorm_kernel(tc, hidden_states, conv_w, norm_w, out):
                             )
                         nc.scalar.copy(out=nw[:, 512 * b2 : 512 * b2 + 512], in_=spread[:])
                 if c in (1, 2) and kind == "P":
-                    for i in PAIR_MX[k]:
+                    for i in PAIR_MX[pairs]:
                         for m in (2 * i, 2 * i + 1):
                             ahead_mx(m, c - 1, 4 * (c - 1) + i)
                         for m in (2 * i + 1, 2 * i):
                             ahead_square(m, c - 1, 4 * (c - 1) + i)
-                    for i in PAIR_SCALE[k]:
+                    for i in PAIR_SCALE[pairs]:
                         for m in (2 * i + 1, 2 * i):
                             ahead_scale(m, c - 1, 4 * (c - 1) + i)
             prev = chunk

@@ -21,10 +21,12 @@ FLOPS = 2 * TOKENS * H * N
 
 TILES = 16
 EARLY = 8
-LAGGED = (0, 1, 2, 3)
+AHEAD = 8
+LAGGED = (0, 1, 2, 3, 4, 5, 6)
 PAIR_MX = {1: (), 2: (0, 1), 3: (2, 3), 4: ()}
 PAIR_SCALE = {1: (), 2: (0, 1), 3: (2, 3), 4: ()}
-PLANS = ("PxPxcsDPP", "DcPPsPP", "DcPPsPP", "DcPPsPDD")
+PLANS = ("PxPxcPDsP", "PDcPsPP", "DcPPsPP", "DcPPsPDD")
+QUANT_AT = ((0, 2), (0, 5))
 
 
 def perm_read(ap, c):
@@ -151,10 +153,10 @@ def tile_conv2dlinalgrmsnorm_kernel(tc, hidden_states, conv_w, norm_w, out):
                 ss[m] = small.tile([P, 2], F32, tag="ss", name="ss%d" % m)
             square(acc[(m, b)][:], ss[m][:, b : b + 1], "junk%d_%d" % (m, b))
 
-        early_ss = [const.tile([P, EARLY], F32, name="early_ss%d" % h) for h in range(2)]
-        early_tot = const.tile([P, EARLY], F32)
+        early_ss = [const.tile([P, AHEAD], F32, name="early_ss%d" % h) for h in range(2)]
+        early_tot = const.tile([P, AHEAD], F32)
         z0 = {}
-        for m in range(EARLY):
+        for m in range(AHEAD):
             z0[m] = const.tile([P, 512], F32, name="z0_%d" % m)
         ahead = {}
 
@@ -206,7 +208,7 @@ def tile_conv2dlinalgrmsnorm_kernel(tc, hidden_states, conv_w, norm_w, out):
 
         def inverse(m):
             rinv[m] = small.tile([P, 1], F32, tag="rinv", name="rinv%d" % m)
-            if m < EARLY:
+            if m < AHEAD:
                 nc.scalar.activation(
                     out=rinv[m][:], in_=ss[m][:, 1:2], func=ACT.Abs_reciprocal_sqrt, bias=early_tot[:, m : m + 1]
                 )
@@ -216,7 +218,7 @@ def tile_conv2dlinalgrmsnorm_kernel(tc, hidden_states, conv_w, norm_w, out):
         def final(m, b):
             if b == 0:
                 osb[m] = outp.tile([P, 1024], F32, tag="osb", name="osb%d" % m)
-                if m < EARLY:
+                if m < AHEAD:
                     if m in LAGGED:
                         nc.vector.tensor_scalar(
                             out=osb[m][:, 0:512],
@@ -327,6 +329,7 @@ def tile_conv2dlinalgrmsnorm_kernel(tc, hidden_states, conv_w, norm_w, out):
                 x_evac(m, False)
 
         prev = None
+        quants = [(m, QUANT_AT[m // 4]) for m in range(EARLY)]
         for c in range(4):
             plan = PLANS[c]
             chunk = {
@@ -340,6 +343,7 @@ def tile_conv2dlinalgrmsnorm_kernel(tc, hidden_states, conv_w, norm_w, out):
             pairs = 0
             opened = False
             held = None
+            lone_raw = None
             tokens = 0
             for k, kind in enumerate(plan):
                 last = k == len(plan) - 1
@@ -353,12 +357,12 @@ def tile_conv2dlinalgrmsnorm_kernel(tc, hidden_states, conv_w, norm_w, out):
                 if kind == "c":
                     raw = w_load(c, layer, 1)
                     lone = bigp.tile([P, 2048], F32, tag="big", name="src%d_%d" % (c, k))
-                    nc.scalar.copy(out=split_write(lone[:], 8), in_=perm_read(raw[:], 8))
+                    nc.scalar.copy(out=split_write(lone[:, 1024:2048], 4), in_=perm_read(raw[:, 1024:2048], 4))
+                    lone_raw = raw
                     layer += 1
                 elif kind == "s":
-                    for beta in range(4):
+                    for beta in (1, 3):
                         w_turn(lone, chunk["banks"], beta, not opened, False)
-                    opened = True
                 elif kind == "D":
                     raw = w_load(c, layer, 1)
                     for beta in range(4):
@@ -371,7 +375,15 @@ def tile_conv2dlinalgrmsnorm_kernel(tc, hidden_states, conv_w, norm_w, out):
                     raw = w_load(c, layer, 2)
                     src = bigp.tile([P, 2048], F32, tag="big", name="src%d_%d" % (c, k))
                     pairs += 1
-                    w_add(src, raw, 4 if c == 3 and pairs == 3 else 1)
+                    w_add(src, raw, 4 if c == 3 and pairs == 3 else 2)
+                    if lone_raw is not None:
+                        nc.vector.tensor_tensor(
+                            out=split_write(src[:, 0:1024], 4),
+                            in0=split_write(src[:, 0:1024], 4),
+                            in1=perm_read(lone_raw[:, 0:1024], 4),
+                            op=ALU.add,
+                        )
+                        lone_raw = None
                     if c == 3 and pairs == 3:
                         held = src
                     else:
@@ -379,14 +391,12 @@ def tile_conv2dlinalgrmsnorm_kernel(tc, hidden_states, conv_w, norm_w, out):
                             w_turn(src, chunk["banks"], beta, not opened, last)
                         opened = True
                     layer += 2
-                    if c == 0:
-                        for m in range(4 * (pairs - 2), 4 * (pairs - 1)):
-                            if 0 <= m < EARLY:
-                                x_quant(m)
+                    while quants and quants[0][1] <= (c, k):
+                        x_quant(quants.pop(0)[0])
                     if pairs == 2 and prev is not None:
                         for beta in range(4):
                             w_quant(prev, beta)
-                if c == 0 and k == 7:
+                if c == 0 and k == len(plan) - 1:
                     nwt = bank(4, "nwt", BF16)
                     nc.tensor.transpose(nwt[:, 0:128], nw_rows[:], ident_bf[:])
                     nw_cols = const.tile([P, 8], F32)
@@ -416,7 +426,7 @@ def tile_conv2dlinalgrmsnorm_kernel(tc, hidden_states, conv_w, norm_w, out):
         for a in range(EARLY // 4, TILES // 4):
             load_x(a)
         early_total()
-        for m in LAGGED[0:2]:
+        for m in LAGGED[0:5]:
             nc.vector.tensor_tensor(out=z0[m][:], in0=z0[m][:], in1=nw[:, 0:512], op=ALU.mult)
         w_evac(chunk, 0, False)
         w_evac(chunk, 1, True)
@@ -427,9 +437,9 @@ def tile_conv2dlinalgrmsnorm_kernel(tc, hidden_states, conv_w, norm_w, out):
         w_quant(chunk, 2)
         w_quant(chunk, 3)
 
-        for m in LAGGED[2:4]:
+        for m in LAGGED[5:]:
             nc.vector.tensor_tensor(out=z0[m][:], in0=z0[m][:], in1=nw[:, 0:512], op=ALU.mult)
-        pending = [(m, b) for m in range(TILES) for b in range(2) if m >= EARLY or b == 1]
+        pending = [(m, b) for m in range(TILES) for b in range(2) if m >= AHEAD or b == 1]
         free = list(range(0, 6))
         begun = []
         while free:
@@ -442,13 +452,13 @@ def tile_conv2dlinalgrmsnorm_kernel(tc, hidden_states, conv_w, norm_w, out):
                     mx_pass(m, b, g)
             x_t(EARLY + (len(few) > 2), 6 + (len(few) > 2))
         for m in range(TILES + 1):
-            if EARLY <= m < TILES:
+            if AHEAD <= m < TILES:
                 sumsq(m, 0)
-                if m > EARLY:
+                if m > AHEAD:
                     inverse(m - 1)
             if m < TILES:
                 sumsq(m, 1)
-            if m < EARLY:
+            if m < AHEAD:
                 inverse(m)
             if m == TILES:
                 inverse(m - 1)
@@ -456,7 +466,7 @@ def tile_conv2dlinalgrmsnorm_kernel(tc, hidden_states, conv_w, norm_w, out):
                 final(m - 1, 0)
                 if m == TILES or m == 1:
                     store(m - 1, 0, 512)
-            if EARLY <= m < TILES:
+            if AHEAD <= m < TILES:
                 total(m)
             if m >= 1:
                 final(m - 1, 1)
@@ -464,7 +474,7 @@ def tile_conv2dlinalgrmsnorm_kernel(tc, hidden_states, conv_w, norm_w, out):
                     store(m - 1, 512, 1024)
                 else:
                     store(m - 1, 0, 1024)
-                if m - 1 >= EARLY:
+                if m - 1 >= AHEAD:
                     free.append(where[(m - 1, 0)])
                 free.append(where[(m - 1, 1)])
             if m >= 2 and EARLY + m - 2 < TILES:

from contextlib import ExitStack

import concourse.mybir as mybir
from concourse.masks import make_identity

F32 = mybir.dt.float32
BF16 = mybir.dt.bfloat16
U32 = mybir.dt.uint32
U8 = mybir.dt.uint8
FP8X4 = mybir.dt.float8_e4m3fn_x4
ALU = mybir.AluOpType
ACT = mybir.ActivationFunctionType

P = 128
H = 1024
N = 1024
L = 10
TOKENS = 2048
EPS = 1e-06
FLOPS = 2 * TOKENS * H * N

TILES = 16
EARLY = 8
AHEAD = 8
LAGGED = (0, 1, 2, 3, 4, 5, 6)
PAIR_MX = {1: (), 2: (0, 1), 3: (2, 3), 4: ()}
PAIR_SCALE = {1: (), 2: (0, 1), 3: (2, 3), 4: ()}
PLANS = ("PxPxcPDsP", "PDcPsPP", "DcPPsPP", "DcPPsPDD")
QUANT_AT = ((0, 2), (0, 5))


def perm_read(ap, c):
    return ap.rearrange("p (c q e) -> p c e q", c=c, q=128, e=2)


def split_write(ap, c):
    return ap.rearrange("p (c e q) -> p c e q", c=c, q=128, e=2)


def tile_conv2dlinalgrmsnorm_kernel(tc, hidden_states, conv_w, norm_w, out):
    nc = tc.nc
    x_flat = hidden_states.flatten_outer_dims()
    out_flat = out.flatten_outer_dims()
    with ExitStack() as ctx:
        const = ctx.enter_context(tc.tile_pool(name="const", bufs=1))
        rawp = ctx.enter_context(tc.tile_pool(name="rawp", bufs=10))
        bigp = ctx.enter_context(tc.tile_pool(name="bigp", bufs=6))
        outp = ctx.enter_context(tc.tile_pool(name="outp", bufs=4))
        grpp = ctx.enter_context(tc.tile_pool(name="grpp", bufs=4))
        xcp = ctx.enter_context(tc.tile_pool(name="xcp", bufs=16))
        junkp = ctx.enter_context(tc.tile_pool(name="junkp", bufs=2))
        small = ctx.enter_context(tc.tile_pool(name="small", bufs=12))
        psum = ctx.enter_context(tc.psum_pool(name="psum", bufs=1))
        ctx.enter_context(tc.manual_schedule())

        def bank(i, name, dtype=F32):
            return psum.tile([P, 512 if dtype == F32 else 1024], dtype, tag="bank%d" % i, name=name)

        xraws = {}

        def load_x(a):
            xraws[a] = rawp.tile([P, 4096], BF16, tag="raw", name="xraw%d" % a)
            nc.sync.dma_start(
                out=xraws[a][:],
                in_=x_flat[512 * a : 512 * a + 512, :].rearrange("(p i) h -> p (i h)", i=4),
            )

        warm = const.tile([P, 1], F32)
        nc.vector.memset(warm[:], 1.0)
        nc.scalar.activation(out=warm[:], in_=warm[:], func=ACT.Abs_reciprocal_sqrt)
        nw_rows = const.tile([P, P], BF16)
        nc.vector.memset(nw_rows[:], 0.0)
        nc.scalar.dma_start(out=nw_rows[0:8, :], in_=norm_w.rearrange("(m j) -> m j", m=8))
        nw = const.tile([P, N], BF16)
        ident = const.tile([P, P], F32)
        make_identity(nc, ident[:])
        ident_bf = const.tile([P, P], BF16)
        make_identity(nc, ident_bf[:])
        wc = {}
        ws = {}
        for b in range(2):
            for g in range(2):
                wc[(b, g)] = const.tile([P, 512], U32, name="wc%d%d" % (b, g), align_bytes=64)
                ws[(b, g)] = const.tile([P, 512], U8, name="ws%d%d" % (b, g), align_bytes=64)

        xt = {}
        xg = {}
        xc = {}
        xs = {}

        def x_t(m, i_bank):
            a, i = divmod(m, 4)
            xw = xraws[a][:].bitcast(F32)
            xt[m] = bank(i_bank, "xt%d" % m)
            for cc in range(4):
                nc.tensor.transpose(
                    xt[m][:, 128 * cc : 128 * cc + 128],
                    xw[:, 512 * i + 128 * cc : 512 * i + 128 * cc + 128],
                    ident[:],
                )

        def x_evac(m, on_vector):
            xg[m] = grpp.tile([P, 1024], BF16, tag="xgrp", name="xg%d" % m, align_bytes=64)
            dst = xg[m][:].bitcast(F32).rearrange("p (g r u) -> p g r u", g=2, u=2)
            src = xt[m][:].rearrange("p (g u r) -> p g r u", g=2, u=2)
            if on_vector:
                nc.vector.tensor_copy(out=dst, in_=src)
            else:
                nc.scalar.copy(out=dst, in_=src)

        def x_quant(m):
            xc[m] = xcp.tile([P, 256], U32, tag="xc", name="xc%d" % m, align_bytes=64)
            xs[m] = xcp.tile([P, 256], U8, tag="xs", name="xs%d" % m, align_bytes=64)
            nc.vector.quantize_mx(out=xc[m][:].bitcast(FP8X4), scales=xs[m][:], in_=xg[m][:])

        acc = {}
        ss = {}
        tot = {}
        rinv = {}
        osb = {}

        where = {}

        def mx_open(m, b, i_bank):
            where[(m, b)] = i_bank
            acc[(m, b)] = bank(i_bank, "acc%d_%d" % (m, b))

        def mx_pass(m, b, g):
            nc.tensor.matmul_mx(
                out=acc[(m, b)][:],
                lhsT=xc[m][:, 128 * g : 128 * g + 128].bitcast(FP8X4),
                lhsT_scale=xs[m][:, 128 * g : 128 * g + 128],
                rhs=wc[(b, g)][:].bitcast(FP8X4),
                rhs_scale=ws[(b, g)][:],
                start=(g == 0),
                stop=(g == 1),
            )

        def mx(m, b, i_bank):
            mx_open(m, b, i_bank)
            for g in range(2):
                mx_pass(m, b, g)

        def square(src, accum, name):
            junk = junkp.tile([P, 512], BF16, tag="junk", name=name)
            width = src.shape[1]
            nc.scalar.activation(
                out=junk[:, 0:width], in_=src, func=ACT.Square, scale=1.0 / 32.0, accum_out=accum
            )

        def sumsq(m, b):
            if m not in ss:
                ss[m] = small.tile([P, 2], F32, tag="ss", name="ss%d" % m)
            square(acc[(m, b)][:], ss[m][:, b : b + 1], "junk%d_%d" % (m, b))

        early_ss = [const.tile([P, AHEAD], F32, name="early_ss%d" % h) for h in range(2)]
        early_tot = const.tile([P, AHEAD], F32)
        z0 = {}
        for m in range(AHEAD):
            z0[m] = const.tile([P, 512], F32, name="z0_%d" % m)
        ahead = {}

        def ahead_mx(m, h, i_bank):
            if m % 2 == 0:
                ahead[i_bank] = bank(i_bank, "ahead%d_%d" % (h, m))
            for g in range(2):
                nc.tensor.matmul_mx(
                    out=ahead[i_bank][:, 256 * (m % 2) : 256 * (m % 2) + 256],
                    lhsT=xc[m][:, 128 * g : 128 * g + 128].bitcast(FP8X4),
                    lhsT_scale=xs[m][:, 128 * g : 128 * g + 128],
                    rhs=wc[(0, g)][:, 256 * h : 256 * h + 256].bitcast(FP8X4),
                    rhs_scale=ws[(0, g)][:, 256 * h : 256 * h + 256],
                    start=(g == 0),
                    stop=(g == 1),
                )

        def ahead_square(m, h, i_bank):
            lo = 256 * (m % 2)
            square(ahead[i_bank][:, lo : lo + 256], early_ss[h][:, m : m + 1], "ajunk%d_%d" % (h, m))

        def ahead_scale(m, h, i_bank):
            lo = 256 * (m % 2)
            nc.scalar.copy(
                out=z0[m][:, 256 * h : 256 * h + 256].rearrange("t (q j) -> t q j", j=2),
                in_=ahead[i_bank][:, lo : lo + 256].rearrange("t (j q) -> t q j", j=2),
            )

        def early_total():
            nc.vector.scalar_tensor_tensor(
                out=early_tot[:],
                in0=early_ss[0][:],
                scalar=EPS * L * L,
                in1=early_ss[1][:],
                op0=ALU.add,
                op1=ALU.add,
            )

        def total(m):
            tot[m] = small.tile([P, 1], F32, tag="tot", name="tot%d" % m)
            nc.vector.tensor_scalar(
                out=tot[m][:],
                in0=ss[m][:, 0:1],
                scalar1=ss[m][:, 1:2],
                scalar2=EPS * L * L,
                op0=ALU.add,
                op1=ALU.add,
            )

        def inverse(m):
            rinv[m] = small.tile([P, 1], F32, tag="rinv", name="rinv%d" % m)
            if m < AHEAD:
                nc.scalar.activation(
                    out=rinv[m][:], in_=ss[m][:, 1:2], func=ACT.Abs_reciprocal_sqrt, bias=early_tot[:, m : m + 1]
                )
            else:
                nc.scalar.activation(out=rinv[m][:], in_=tot[m][:], func=ACT.Abs_reciprocal_sqrt)

        def final(m, b):
            if b == 0:
                osb[m] = outp.tile([P, 1024], F32, tag="osb", name="osb%d" % m)
                if m < AHEAD:
                    if m in LAGGED:
                        nc.vector.tensor_scalar(
                            out=osb[m][:, 0:512],
                            in0=z0[m][:],
                            scalar1=rinv[m][:, 0:1],
                            scalar2=None,
                            op0=ALU.mult,
                        )
                    else:
                        nc.vector.scalar_tensor_tensor(
                            out=osb[m][:, 0:512],
                            in0=z0[m][:],
                            scalar=rinv[m][:, 0:1],
                            in1=nw[:, 0:512],
                            op0=ALU.mult,
                            op1=ALU.mult,
                        )
                    return
            width = 256 if b == 0 else 512
            for lo in range(0, 512, width):
                at = 512 * b + lo
                nc.vector.scalar_tensor_tensor(
                    out=osb[m][:, at : at + width].rearrange("t (q j) -> t q j", j=2),
                    in0=acc[(m, b)][:, lo : lo + width].rearrange("t (j q) -> t q j", j=2),
                    scalar=rinv[m][:, 0:1],
                    in1=nw[:, at : at + width].rearrange("t (q j) -> t q j", j=2),
                    op0=ALU.mult,
                    op1=ALU.mult,
                )

        def store(m, lo, hi):
            a, i = divmod(m, 4)
            nc.sync.dma_start(
                out=out_flat[512 * a : 512 * a + 512, :].rearrange("(p i) n -> p i n", i=4)[:, i, lo:hi],
                in_=osb[m][:, lo:hi],
            )

        def block(raw, row, g, t):
            base = row * 1024 + g * 512 + (t // 2) * 256
            return raw[:, base : base + 256].rearrange("p (q e) -> p e q", e=2)[:, t % 2, :]

        def w_direct(raw, banks, beta, first):
            g, j = divmod(beta, 2)
            for t in range(4):
                nc.tensor.matmul(
                    out=banks[beta][:, 128 * t : 128 * t + 128],
                    lhsT=block(raw, j, g, t),
                    rhs=ident_bf[:],
                    start=(first and t == 0),
                    stop=False,
                )

        def w_turn(src, banks, beta, first, last):
            g, j = divmod(beta, 2)
            for t in range(4):
                col = (j * 8 + g * 4 + t) * 128
                nc.tensor.matmul(
                    out=banks[beta][:, 128 * t : 128 * t + 128],
                    lhsT=src[:, col : col + 128],
                    rhs=ident[:],
                    start=(first and t == 0),
                    stop=(last and t == 3),
                    is_transpose=True,
                )

        def w_evac(chunk, beta, on_vector):
            g, j = divmod(beta, 2)
            dst = chunk["groups"][g][:, 512 * j : 512 * j + 512].rearrange("p (n t) -> p n t", t=4)
            src = chunk["banks"][beta][:].rearrange("p (t n) -> p n t", t=4)
            if on_vector:
                nc.vector.tensor_copy(out=dst, in_=src)
            else:
                nc.scalar.copy(out=dst, in_=src)

        def w_quant(chunk, beta):
            g, j = divmod(beta, 2)
            b, jp = divmod(chunk["c"], 2)
            lo = 256 * jp + 128 * j if b == 0 else 256 * j + 128 * jp
            nc.vector.quantize_mx(
                out=wc[(b, g)][:, lo : lo + 128].bitcast(FP8X4),
                scales=ws[(b, g)][:, lo : lo + 128],
                in_=chunk["groups"][g][:, 512 * j : 512 * j + 512],
            )

        def w_load(c, l0, n_l):
            raw = rawp.tile([P, 2048 * n_l], BF16, tag="raw", name="raw%d_%d" % (c, l0))
            nc.sync.dma_start(
                out=raw[:].rearrange("p (l c) -> p l c", l=n_l),
                in_=conv_w[l0 : l0 + n_l, 256 * c : 256 * c + 256, :].rearrange("l (p j) h -> p l (j h)", j=2),
            )
            return raw

        def w_add(dst, raw, parts):
            width = 2048 // parts
            for lo in range(0, 2048, width):
                nc.vector.tensor_tensor(
                    out=split_write(dst[:, lo : lo + width], width // 256),
                    in0=perm_read(raw[:, lo : lo + width], width // 256),
                    in1=perm_read(raw[:, 2048 + lo : 2048 + lo + width], width // 256),
                    op=ALU.add,
                )

        def prepare(a):
            load_x(a)
            for i in range(4):
                m = 4 * a + i
                x_t(m, 4 + m % 4)
                x_evac(m, False)

        prev = None
        quants = [(m, QUANT_AT[m // 4]) for m in range(EARLY)]
        for c in range(4):
            plan = PLANS[c]
            chunk = {
                "c": c,
                "banks": [bank(4 * (c % 2) + beta, "wb%d_%d" % (c, beta)) for beta in range(4)],
                "groups": [
                    grpp.tile([P, 1024], BF16, tag="wgrp", name="wg%d_%d" % (c, g), align_bytes=64) for g in range(2)
                ],
            }
            layer = 0
            pairs = 0
            opened = False
            held = None
            lone_raw = None
            tokens = 0
            for k, kind in enumerate(plan):
                last = k == len(plan) - 1
                if kind == "x":
                    prepare(tokens)
                    tokens += 1
                    continue
                if k == 1 and prev is not None:
                    for beta in range(4):
                        w_evac(prev, beta, False)
                if kind == "c":
                    raw = w_load(c, layer, 1)
                    lone = bigp.tile([P, 2048], F32, tag="big", name="src%d_%d" % (c, k))
                    nc.scalar.copy(out=split_write(lone[:, 1024:2048], 4), in_=perm_read(raw[:, 1024:2048], 4))
                    lone_raw = raw
                    layer += 1
                elif kind == "s":
                    for beta in (1, 3):
                        w_turn(lone, chunk["banks"], beta, not opened, False)
                elif kind == "D":
                    raw = w_load(c, layer, 1)
                    for beta in range(4):
                        w_direct(raw, chunk["banks"], beta, not opened)
                        if last:
                            w_turn(held, chunk["banks"], beta, False, True)
                    opened = True
                    layer += 1
                else:
                    raw = w_load(c, layer, 2)
                    src = bigp.tile([P, 2048], F32, tag="big", name="src%d_%d" % (c, k))
                    pairs += 1
                    w_add(src, raw, 4 if c == 3 and pairs == 3 else 2)
                    if lone_raw is not None:
                        nc.vector.tensor_tensor(
                            out=split_write(src[:, 0:1024], 4),
                            in0=split_write(src[:, 0:1024], 4),
                            in1=perm_read(lone_raw[:, 0:1024], 4),
                            op=ALU.add,
                        )
                        lone_raw = None
                    if c == 3 and pairs == 3:
                        held = src
                    else:
                        for beta in range(4):
                            w_turn(src, chunk["banks"], beta, not opened, last)
                        opened = True
                    layer += 2
                    while quants and quants[0][1] <= (c, k):
                        x_quant(quants.pop(0)[0])
                    if pairs == 2 and prev is not None:
                        for beta in range(4):
                            w_quant(prev, beta)
                if c == 0 and k == len(plan) - 1:
                    nwt = bank(4, "nwt", BF16)
                    nc.tensor.transpose(nwt[:, 0:128], nw_rows[:], ident_bf[:])
                    nw_cols = const.tile([P, 8], F32)
                    nc.scalar.copy(out=nw_cols[:], in_=nwt[:, 0:8])
                    for b2 in range(2):
                        spread = bank(5 + b2, "spread%d" % b2)
                        for m in range(4):
                            nc.tensor.matmul(
                                out=spread[:, 128 * m : 128 * m + 128],
                                lhsT=nw_cols[:, 4 * b2 + m : 4 * b2 + m + 1].to_broadcast([P, P]),
                                rhs=ident[:],
                                start=True,
                                stop=True,
                                is_transpose=True,
                            )
                        nc.scalar.copy(out=nw[:, 512 * b2 : 512 * b2 + 512], in_=spread[:])
                if c in (1, 2) and kind == "P":
                    for i in PAIR_MX[pairs]:
                        for m in (2 * i, 2 * i + 1):
                            ahead_mx(m, c - 1, 4 * (c - 1) + i)
                        for m in (2 * i + 1, 2 * i):
                            ahead_square(m, c - 1, 4 * (c - 1) + i)
                    for i in PAIR_SCALE[pairs]:
                        for m in (2 * i + 1, 2 * i):
                            ahead_scale(m, c - 1, 4 * (c - 1) + i)
            prev = chunk
        for a in range(EARLY // 4, TILES // 4):
            load_x(a)
        early_total()
        for m in LAGGED[0:5]:
            nc.vector.tensor_tensor(out=z0[m][:], in0=z0[m][:], in1=nw[:, 0:512], op=ALU.mult)
        w_evac(chunk, 0, False)
        w_evac(chunk, 1, True)
        w_quant(chunk, 0)
        w_evac(chunk, 2, False)
        w_quant(chunk, 1)
        w_evac(chunk, 3, False)
        w_quant(chunk, 2)
        w_quant(chunk, 3)

        for m in LAGGED[5:]:
            nc.vector.tensor_tensor(out=z0[m][:], in0=z0[m][:], in1=nw[:, 0:512], op=ALU.mult)
        pending = [(m, b) for m in range(TILES) for b in range(2) if m >= AHEAD or b == 1]
        free = list(range(0, 6))
        begun = []
        while free:
            m, b = pending.pop(0)
            mx_open(m, b, free.pop(0))
            begun.append((m, b))
        for few in (begun[:2], begun[2:]):
            for g in range(2):
                for m, b in few:
                    mx_pass(m, b, g)
            x_t(EARLY + (len(few) > 2), 6 + (len(few) > 2))
        for m in range(TILES + 1):
            if AHEAD <= m < TILES:
                sumsq(m, 0)
                if m > AHEAD:
                    inverse(m - 1)
            if m < TILES:
                sumsq(m, 1)
            if m < AHEAD:
                inverse(m)
            if m == TILES:
                inverse(m - 1)
            if m >= 1:
                final(m - 1, 0)
                if m == TILES or m == 1:
                    store(m - 1, 0, 512)
            if AHEAD <= m < TILES:
                total(m)
            if m >= 1:
                final(m - 1, 1)
                if m == TILES or m == 1:
                    store(m - 1, 512, 1024)
                else:
                    store(m - 1, 0, 1024)
                if m - 1 >= AHEAD:
                    free.append(where[(m - 1, 0)])
                free.append(where[(m - 1, 1)])
            if m >= 2 and EARLY + m - 2 < TILES:
                x_quant(EARLY + m - 2)
            if m >= 1 and EARLY + m - 1 < TILES:
                x_evac(EARLY + m - 1, m % 4 == 3)
                if EARLY + m + 1 < TILES:
                    x_t(EARLY + m + 1, 6 + (m - 1) % 2)
            while free and pending and pending[0][0] in xc:
                mx(pending[0][0], pending[0][1], free.pop(0))
                pending.pop(0)
